import numpy as np
import ml_dtypes


def mxq(x, axis, fmt="e4m3"):
    dtype, down = {"e4m3": (ml_dtypes.float8_e4m3fn, 7), "e5m2": (ml_dtypes.float8_e5m2, 14)}[fmt]
    v = np.moveaxis(np.asarray(x, np.float32).astype(ml_dtypes.bfloat16).astype(np.float64), axis, -1)
    blocks = v.reshape(v.shape[:-1] + (-1, 32))
    amax = np.abs(blocks).max(-1, keepdims=True)
    byte = np.maximum(np.where(amax > 0, np.frexp(amax)[1] - 1 + 127, 0) - down, 1)
    scale = np.exp2(byte - 127.0)
    codes = (blocks / scale).astype(np.float32).astype(dtype).astype(np.float64)
    return np.moveaxis((codes * scale).reshape(v.shape), -1, axis)


WIDE = False


def mx_kscale(k):
    if not WIDE:
        return np.ones(k)
    levels = np.array([10, -10, 5, -5, 0])
    a = np.random.permutation(np.resize(levels, k // 512 * 4)).reshape(k // 512, 4)
    idx = np.arange(k)
    return np.exp2(a[idx // 512, idx % 128 // 32])


BF16 = ml_dtypes.bfloat16


def bf(x):
    return np.asarray(x, np.float32).astype(BF16)


def f64(x):
    return np.asarray(x).astype(np.float64)


B, N, H = 6, 1024, 512
BN_EPS = 1e-5


def setup_inputs():
    s = mx_kscale(H)
    return {"h": bf(np.random.standard_normal((B, N, H)) * s),
            "adj": bf(np.random.random_sample((B, N, N))),
            "W": bf(np.random.standard_normal((H, H)) * 2.0 / np.sqrt(H) / s[None, :]),
            "b": bf(np.random.standard_normal(H) * 1.0),
            "bn_weight": bf(1.0 + 0.1 * np.random.standard_normal(H)),
            "bn_bias": bf(0.1 * np.random.standard_normal(H)),
            "res_weight": bf((0.3 + 0.1 * np.random.standard_normal(1)) / s.max())}


def reference(h, adj, W, b, bn_weight, bn_bias, res_weight):
    h = f64(h)
    A = f64(adj) + np.eye(N)
    deg = A.sum(axis=-1)
    dis = deg ** -0.5
    dis = np.where(np.isinf(dis), 0.0, dis)
    A_hat = dis[:, :, None] * A * dis[:, None, :]
    h_lin = (mxq(h, 2, "e4m3") @ mxq(f64(W), 1, "e4m3").T) + f64(b)
    out = mxq(A_hat, 2, "e4m3") @ mxq(h_lin, 1, "e4m3")
    flat = out.reshape(B * N, H)
    mean = flat.mean(axis=0)
    var = flat.var(axis=0)
    flat = (flat - mean) * (1.0 / np.sqrt(var + BN_EPS)) * f64(bn_weight) + f64(bn_bias)
    out = flat.reshape(B, N, H)
    out = np.maximum(out, 0.0)
    return out + f64(res_weight) * h

@@ -1,0 +1,431 @@
+from contextlib import ExitStack
+
+import concourse.mybir as mybir
+from concourse.masks import make_identity
+
+FLOPS = 2 * 6144 * 512 * 512 + 2 * 6 * 1024 * 1024 * 512
+
+F32 = mybir.dt.float32
+BF16 = mybir.dt.bfloat16
+U32 = mybir.dt.uint32
+U8 = mybir.dt.uint8
+FP8X4 = mybir.dt.float8_e4m3fn_x4
+ALU = mybir.AluOpType
+ACT = mybir.ActivationFunctionType
+AX = mybir.AxisListType
+
+P = 128
+G = 6
+N = 1024
+H = 512
+SLOT = 16384
+BN_EPS = 1e-5
+
+
+def tile_gcnlayer_t_kernel(tc, h, adj, W, b, bn_weight, bn_bias, res_weight, out):
+    nc = tc.nc
+    with ExitStack() as ctx:
+        const = ctx.enter_context(tc.tile_pool(name="const", bufs=1))
+        big = ctx.enter_context(tc.tile_pool(name="big", bufs=1))
+        work = ctx.enter_context(tc.tile_pool(name="work", bufs=2))
+        small = ctx.enter_context(tc.tile_pool(name="small", bufs=2))
+
+        ident_bf = const.tile([P, P], BF16, name="ident_bf")
+        make_identity(nc, ident_bf[:])
+        ident_f = const.tile([P, P], F32, name="ident_f")
+        make_identity(nc, ident_f[:])
+
+        vt = const.tile([P, P], BF16, name="vt")
+        nc.vector.memset(vt[:], 0.0)
+        warm = const.tile([P, 1], F32, name="warm")
+        nc.vector.memset(warm[:], 1.0)
+        nc.scalar.activation(out=warm[:], in_=warm[:], func=ACT.Sqrt)
+
+        w_sb = work.tile([P, 4, H], BF16, tag="hlg", align_bytes=64)
+        nc.sync.dma_start(out=w_sb[:], in_=W.rearrange("(a p) k -> p a k", p=P))
+        b_all = const.tile([P, H], BF16, name="b_all")
+        nc.scalar.dma_start(out=b_all[:], in_=b.partition_broadcast(P))
+        nc.scalar.dma_start(out=vt[0:4, :], in_=bn_weight.rearrange("(a p) -> a p", p=P))
+        nc.scalar.dma_start(out=vt[4:8, :], in_=bn_bias.rearrange("(a p) -> a p", p=P))
+        rw_bf = const.tile([P, 1], BF16, name="rw_bf")
+        nc.scalar.dma_start(out=rw_bf[:], in_=res_weight.partition_broadcast(P))
+
+        h_sb = const.tile([P, G * 8, H], BF16, name="h_sb")
+        adj_t = []
+        y_t = []
+        for g in range(G):
+            nc.sync.dma_start(
+                out=h_sb[:, 8 * g : 8 * g + 8, :], in_=h[g].rearrange("(t p) k -> p t k", p=P)
+            )
+            a_tile = big.tile([P, 8, N], BF16, name="adj%d" % g, offset=(g + 1) * SLOT)
+            adj_t.append(a_tile)
+            for hf in range(2):
+                nc.sync.dma_start(
+                    out=a_tile[:, 4 * hf : 4 * hf + 4, :],
+                    in_=adj[g, 512 * hf : 512 * hf + 512, :].rearrange("(t p) n -> p t n", p=P),
+                )
+
+        wc = const.tile([P, H], U32, name="wc", align_bytes=64)
+        ws = const.tile([P, H], U8, name="ws", align_bytes=64)
+        ysum = const.tile([P, 48], F32, name="ysum")
+        ysq = const.tile([P, 48], F32, name="ysq")
+        negs = const.tile([P, 4], F32, name="negs")
+        negr = const.tile([P, 4], F32, name="negr")
+        bnv = const.tile([P, 8], F32, name="bnv")
+        rw = const.tile([P, 1], F32, name="rw")
+        nc.vector.tensor_copy(out=rw[:], in_=rw_bf[:])
+
+        state = {}
+
+        with tc.psum_pool(name="ps1", bufs=2) as psum:
+            tpv = psum.tile([P, 8, P], BF16, tag="tp")
+            nc.tensor.transpose(tpv[:, 0, :], vt[:], ident_bf[:])
+            nc.vector.tensor_copy(out=bnv[:], in_=tpv[:, 0, 0:8])
+
+            def words_to_k(src_tiles, dst):
+                dstf = dst[:].bitcast(F32).rearrange("p (a n u) -> p a n u", a=4, u=2)
+                for pr in range(2):
+                    ps = psum.tile([P, 2, 2, P], F32, tag="tp")
+                    for a2 in range(2):
+                        for u in range(2):
+                            nc.tensor.transpose(
+                                ps[:, a2, u, :],
+                                src_tiles[2 * pr + a2].bitcast(F32)[:, P * u : P * u + P],
+                                ident_f[:],
+                            )
+                    nc.scalar.copy(
+                        out=dstf[:, 2 * pr : 2 * pr + 2], in_=ps[:].rearrange("p a u n -> p a n u")
+                    )
+
+            wg = work.tile([P, 4 * H], BF16, tag="hg", align_bytes=64)
+            words_to_k([w_sb[:, a, :] for a in range(4)], wg)
+            nc.vector.quantize_mx(out=wc[:].bitcast(FP8X4), scales=ws[:], in_=wg[:])
+
+            def h_transpose(g, c):
+                hg = work.tile([P, 4 * H], BF16, tag="hg", align_bytes=64)
+                words_to_k([h_sb[:, 8 * g + 4 * c + t, :] for t in range(4)], hg)
+                state[("hg", g, c)] = hg
+
+            def h_quant(g, c):
+                hc = work.tile([P, H], U32, tag="hc", align_bytes=64)
+                hs = work.tile([P, H], U8, tag="hs", align_bytes=64)
+                nc.vector.quantize_mx(
+                    out=hc[:].bitcast(FP8X4), scales=hs[:], in_=state[("hg", g, c)][:]
+                )
+                state[("hc", g, c)] = (hc, hs)
+
+            def mm1(g, c, fc):
+                if fc == 0:
+                    hlg_new = work.tile([P, 4 * H], BF16, tag="hlg", align_bytes=64)
+                    state[("hlg", g, c)] = hlg_new
+                hlg = state[("hlg", g, c)]
+                hc, hs = state[("hc", g, c)]
+                m1 = psum.tile([P, 4, P], F32, tag="m1")
+                fs = slice(P * fc, P * fc + P)
+                for t in range(4):
+                    ts = slice(P * t, P * t + P)
+                    nc.tensor.matmul_mx(
+                        out=m1[:, t, :],
+                        lhsT=hc[:, ts].bitcast(FP8X4),
+                        lhsT_scale=hs[:, ts],
+                        rhs=wc[:, fs].bitcast(FP8X4),
+                        rhs_scale=ws[:, fs],
+                        start=True,
+                        stop=True,
+                    )
+                nc.vector.tensor_tensor(
+                    out=hlg[:].rearrange("p (f t) -> p f t", t=4)[:, fs, :],
+                    in0=m1[:].rearrange("p t f -> p f t"),
+                    in1=b_all[:, fs].unsqueeze(2).to_broadcast([P, P, 4]),
+                    op=ALU.add,
+                )
+
+            def hl_quant(g, c):
+                if c == 0:
+                    hlc_new = work.tile([P, 2, H], U32, tag="hlc", align_bytes=64)
+                    hls_new = work.tile([P, 2, H], U8, tag="hls", align_bytes=64)
+                    state[("hlc", g)] = (hlc_new, hls_new)
+                hlc, hls = state[("hlc", g)]
+                nc.vector.quantize_mx(
+                    out=hlc[:, c, :].bitcast(FP8X4), scales=hls[:, c, :], in_=state[("hlg", g, c)][:]
+                )
+
+            def deg_row(g, rt):
+                if rt == 0:
+                    deg_new = small.tile([P, 8], F32, tag="deg")
+                    state[("deg", g)] = deg_new
+                deg = state[("deg", g)]
+                src = adj_t[g]
+                if g % 2 == 0:
+                    junk = work.tile([P, N], BF16, tag="junkd", bufs=1)
+                    nc.vector.tensor_scalar(
+                        out=junk[:],
+                        in0=src[:, rt, :],
+                        scalar1=1.0,
+                        scalar2=None,
+                        op0=ALU.mult,
+                        op1=ALU.add,
+                        accum_out=deg[:, rt : rt + 1],
+                    )
+                else:
+                    junk2 = work.tile([P, H], F32, tag="junkd", bufs=1)
+                    nc.vector.scalar_tensor_tensor(
+                        out=junk2[:],
+                        in0=src[:, rt, 0:H],
+                        scalar=1.0,
+                        in1=src[:, rt, H:N],
+                        op0=ALU.mult,
+                        op1=ALU.add,
+                        accum_out=deg[:, rt : rt + 1],
+                    )
+
+            def dis_chain(g):
+                deg = state[("deg", g)]
+                t0 = small.tile([P, 8], F32, tag="t0")
+                nc.vector.tensor_scalar(
+                    out=t0[:], in0=deg[:], scalar1=1.0, scalar2=1e-30, op0=ALU.add, op1=ALU.max
+                )
+                mk = small.tile([P, 8], F32, tag="mk")
+                nc.vector.tensor_scalar(
+                    out=mk[:], in0=deg[:], scalar1=1.0, scalar2=0.0, op0=ALU.add, op1=ALU.is_gt
+                )
+                sq = small.tile([P, 8], F32, tag="sq")
+                nc.scalar.activation(out=sq[:], in_=t0[:], func=ACT.Sqrt)
+                r0 = small.tile([P, 8], F32, tag="r0")
+                nc.vector.reciprocal(out=r0[:], in_=sq[:])
+                n1 = small.tile([P, 8], F32, tag="n1")
+                nc.vector.tensor_tensor(out=n1[:], in0=r0[:], in1=r0[:], op=ALU.mult)
+                n2 = small.tile([P, 8], F32, tag="n2")
+                nc.vector.tensor_tensor(out=n2[:], in0=n1[:], in1=t0[:], op=ALU.mult)
+                n3 = small.tile([P, 8], F32, tag="n3")
+                nc.vector.tensor_scalar(
+                    out=n3[:], in0=n2[:], scalar1=-0.5, scalar2=1.5, op0=ALU.mult, op1=ALU.add
+                )
+                n4 = small.tile([P, 8], F32, tag="n4")
+                nc.vector.tensor_tensor(out=n4[:], in0=r0[:], in1=n3[:], op=ALU.mult)
+                dis = small.tile([P, 8], F32, tag="dis")
+                nc.vector.tensor_tensor(out=dis[:], in0=n4[:], in1=mk[:], op=ALU.mult)
+                state[("dis", g)] = dis
+
+            def dis_spread(g):
+                dis = state[("dis", g)]
+                halves = []
+                for hf in range(2):
+                    ds = psum.tile([P, H], F32, tag="ds")
+                    for r in range(4):
+                        rt = 4 * hf + r
+                        nc.tensor.transpose(
+                            ds[:, P * r : P * r + P],
+                            dis[:, rt : rt + 1].to_broadcast([P, P]),
+                            ident_f[:],
+                        )
+                    halves.append(ds)
+                state[("ds", g)] = halves
+
+            def diag_block(g, rt):
+                a32 = work.tile([P, P], F32, tag="a32", bufs=4)
+                nc.gpsimd.tensor_tensor(
+                    out=a32[:], in0=adj_t[g][:, rt, P * rt : P * rt + P], in1=ident_bf[:], op=ALU.add
+                )
+                state[("a32", g, rt)] = a32
+
+            def a_scale(g, rt):
+                dis = state[("dis", g)]
+                halves = state[("ds", g)]
+                ah = work.tile([P, N], BF16, tag="ah", bufs=3)
+                cuts = sorted(set([0, P * rt, P * rt + P, H, N]))
+                for lo, hi in zip(cuts[:-1], cuts[1:]):
+                    if lo == P * rt:
+                        src = state[("a32", g, rt)][:]
+                    else:
+                        src = adj_t[g][:, rt, lo:hi]
+                    nc.vector.scalar_tensor_tensor(
+                        out=ah[:, lo:hi],
+                        in0=src,
+                        scalar=dis[:, rt : rt + 1],
+                        in1=halves[lo // H][:, lo % H : lo % H + hi - lo],
+                        op0=ALU.mult,
+                        op1=ALU.mult,
+                    )
+                tp = psum.tile([P, 8, P], BF16, tag="tp")
+                for s in range(8):
+                    nc.tensor.transpose(tp[:, s, :], ah[:, P * s : P * s + P], ident_bf[:])
+                ag = work.tile([P, 2, P, 4], BF16, tag="ag", bufs=3, align_bytes=64)
+                nc.scalar.copy(out=ag[:], in_=tp[:].rearrange("p (c t) m -> p c m t", c=2))
+                state[("ag", g, rt)] = ag
+
+            def a_quant(g, rt):
+                r = rt % 4
+                if r == 0:
+                    ac_new = work.tile([P, 2, H], U32, tag="ac", align_bytes=64)
+                    as_new = work.tile([P, 2, H], U8, tag="as", align_bytes=64)
+                    state[("ac", g, rt // 4)] = (ac_new, as_new)
+                ac, asc = state[("ac", g, rt // 4)]
+                ag = state[("ag", g, rt)]
+                for c in range(2):
+                    nc.vector.quantize_mx(
+                        out=ac[:, c, P * r : P * r + P].bitcast(FP8X4),
+                        scales=asc[:, c, P * r : P * r + P],
+                        in_=ag[:, c].rearrange("p m t -> p (m t)"),
+                    )
+
+            def mm2(g, mh):
+                if mh == 0:
+                    y_new = big.tile([P, 4, N], F32, name="y%d" % g, offset=g * SLOT)
+                    y_t.append(y_new)
+                y = y_t[g]
+                ac, asc = state[("ac", g, mh)]
+                hlc, hls = state[("hlc", g)]
+                for fc in range(4):
+                    fs = slice(P * fc, P * fc + P)
+                    m2 = psum.tile([P, H], F32, tag="m2")
+                    for c in range(2):
+                        nc.tensor.matmul_mx(
+                            out=m2[:],
+                            lhsT=hlc[:, c, fs].bitcast(FP8X4),
+                            lhsT_scale=hls[:, c, fs],
+                            rhs=ac[:, c, :].bitcast(FP8X4),
+                            rhs_scale=asc[:, c, :],
+                            start=(c == 0),
+                            stop=(c == 1),
+                        )
+                    if g == 0 and mh == 0:
+                        nc.vector.tensor_reduce(
+                            out=negr[:, fc : fc + 1], in_=m2[:], axis=AX.X, op=ALU.add
+                        )
+                        nc.vector.tensor_scalar(
+                            out=negs[:, fc : fc + 1],
+                            in0=negr[:, fc : fc + 1],
+                            scalar1=-1.0 / H,
+                            scalar2=None,
+                            op0=ALU.mult,
+                        )
+                    idx = 12 * fc + 2 * g + mh
+                    nc.scalar.activation(
+                        out=y[:, fc, H * mh : H * mh + H],
+                        in_=m2[:],
+                        func=ACT.Identity,
+                        bias=negs[:, fc : fc + 1],
+                        scale=1.0,
+                        accum_out=ysum[:, idx : idx + 1],
+                    )
+                    junks = work.tile([P, H], BF16, tag="junks", bufs=1)
+                    nc.scalar.activation(
+                        out=junks[:],
+                        in_=m2[:],
+                        func=ACT.Square,
+                        bias=negs[:, fc : fc + 1],
+                        scale=1.0,
+                        accum_out=ysq[:, idx : idx + 1],
+                    )
+
+            def side_unit(g, i):
+                if i == 0:
+                    h_transpose(g, 0)
+                elif i == 1:
+                    h_quant(g, 0)
+                    h_transpose(g, 1)
+                elif i == 2:
+                    mm1(g, 0, 0)
+                    mm1(g, 0, 1)
+                    h_quant(g, 1)
+                elif i == 3:
+                    mm1(g, 0, 2)
+                    mm1(g, 0, 3)
+                elif i == 4:
+                    hl_quant(g, 0)
+                    mm1(g, 1, 0)
+                    mm1(g, 1, 1)
+                elif i == 5:
+                    mm1(g, 1, 2)
+                    mm1(g, 1, 3)
+                elif i == 6:
+                    hl_quant(g, 1)
+                if i < 6:
+                    deg_row(g, i)
+                elif i == 6:
+                    deg_row(g, 6)
+                    deg_row(g, 7)
+                else:
+                    dis_chain(g)
+
+            for i in range(8):
+                side_unit(0, i)
+            for g in range(G):
+                dis_spread(g)
+                diag_block(g, 0)
+                diag_block(g, 1)
+                for rt in range(8):
+                    if rt + 2 < 8:
+                        diag_block(g, rt + 2)
+                    a_scale(g, rt)
+                    if rt >= 1:
+                        a_quant(g, rt - 1)
+                    if rt == 4:
+                        mm2(g, 0)
+                    if g + 1 < G:
+                        side_unit(g + 1, rt)
+                a_quant(g, 7)
+                mm2(g, 1)
+
+        inv_n = 1.0 / (G * N)
+        s1 = small.tile([P, 4], F32, tag="s1")
+        nc.vector.tensor_reduce(
+            out=s1[:], in_=ysum[:].rearrange("p (f j) -> p f j", f=4), axis=AX.X, op=ALU.add
+        )
+        s2 = small.tile([P, 4], F32, tag="s2")
+        nc.vector.tensor_reduce(
+            out=s2[:], in_=ysq[:].rearrange("p (f j) -> p f j", f=4), axis=AX.X, op=ALU.add
+        )
+        mean = small.tile([P, 4], F32, tag="mean")
+        nc.vector.tensor_scalar(out=mean[:], in0=s1[:], scalar1=inv_n, scalar2=None, op0=ALU.mult)
+        ex2 = small.tile([P, 4], F32, tag="ex2")
+        nc.vector.tensor_scalar(
+            out=ex2[:], in0=s2[:], scalar1=inv_n, scalar2=BN_EPS, op0=ALU.mult, op1=ALU.add
+        )
+        msq = small.tile([P, 4], F32, tag="msq")
+        nc.vector.tensor_tensor(out=msq[:], in0=mean[:], in1=mean[:], op=ALU.mult)
+        vpe = small.tile([P, 4], F32, tag="vpe")
+        nc.vector.tensor_tensor(out=vpe[:], in0=ex2[:], in1=msq[:], op=ALU.subtract)
+        std = small.tile([P, 4], F32, tag="std")
+        nc.scalar.activation(out=std[:], in_=vpe[:], func=ACT.Sqrt)
+        rstd = small.tile([P, 4], F32, tag="rstd")
+        nc.vector.reciprocal(out=rstd[:], in_=std[:])
+        sc = small.tile([P, 4], F32, tag="sc")
+        nc.vector.tensor_tensor(out=sc[:], in0=rstd[:], in1=bnv[:, 0:4], op=ALU.mult)
+        msc = small.tile([P, 4], F32, tag="msc")
+        nc.vector.tensor_tensor(out=msc[:], in0=mean[:], in1=sc[:], op=ALU.mult)
+        sh = small.tile([P, 4], F32, tag="sh")
+        nc.vector.tensor_tensor(out=sh[:], in0=bnv[:, 4:8], in1=msc[:], op=ALU.subtract)
+
+        with tc.psum_pool(name="ps2", bufs=4) as psum2:
+            for g in range(G):
+                y = y_t[g]
+                for mh in range(2):
+                    for fc in range(4):
+                        part = y[:, fc, H * mh : H * mh + H]
+                        nc.scalar.activation(
+                            out=part,
+                            in_=part,
+                            func=ACT.Relu,
+                            bias=sh[:, fc : fc + 1],
+                            scale=sc[:, fc : fc + 1],
+                        )
+                    for r in range(4):
+                        rt = 4 * mh + r
+                        to = psum2.tile([P, H], F32, tag="to")
+                        for fc in range(4):
+                            nc.tensor.transpose(
+                                to[:, P * fc : P * fc + P], y[:, fc, P * rt : P * rt + P], ident_f[:]
+                            )
+                        i = 8 * g + rt
+                        ot = big.tile([P, H], F32, name="ot%d" % i, offset=6 * SLOT + (i % 8) * 2048)
+                        nc.vector.scalar_tensor_tensor(
+                            out=ot[:],
+                            in0=h_sb[:, i, :],
+                            scalar=rw[:, 0:1],
+                            in1=to[:],
+                            op0=ALU.mult,
+                            op1=ALU.add,
+                        )
+                        nc.sync.dma_start(out=out[g, P * rt : P * rt + P, :], in_=ot[:])

@@ -25,86 +25,158 @@ BN_EPS = 1e-5
 def tile_gcnlayer_t_kernel(tc, h, adj, W, b, bn_weight, bn_bias, res_weight, out):
     nc = tc.nc
     with ExitStack() as ctx:
+        ctx.enter_context(tc.manual_schedule())
         const = ctx.enter_context(tc.tile_pool(name="const", bufs=1))
         big = ctx.enter_context(tc.tile_pool(name="big", bufs=1))
         work = ctx.enter_context(tc.tile_pool(name="work", bufs=2))
         small = ctx.enter_context(tc.tile_pool(name="small", bufs=2))
 
-        ident_bf = const.tile([P, P], BF16, name="ident_bf")
-        make_identity(nc, ident_bf[:])
-        ident_f = const.tile([P, P], F32, name="ident_f")
-        make_identity(nc, ident_f[:])
-
-        vt = const.tile([P, P], BF16, name="vt")
-        nc.vector.memset(vt[:], 0.0)
-        warm = const.tile([P, 1], F32, name="warm")
-        nc.vector.memset(warm[:], 1.0)
-        nc.scalar.activation(out=warm[:], in_=warm[:], func=ACT.Sqrt)
-
-        w_sb = work.tile([P, 4, H], BF16, tag="hlg", align_bytes=64)
-        nc.sync.dma_start(out=w_sb[:], in_=W.rearrange("(a p) k -> p a k", p=P))
-        b_all = const.tile([P, H], BF16, name="b_all")
-        nc.scalar.dma_start(out=b_all[:], in_=b.partition_broadcast(P))
-        nc.scalar.dma_start(out=vt[0:4, :], in_=bn_weight.rearrange("(a p) -> a p", p=P))
-        nc.scalar.dma_start(out=vt[4:8, :], in_=bn_bias.rearrange("(a p) -> a p", p=P))
-        rw_bf = const.tile([P, 1], BF16, name="rw_bf")
-        nc.scalar.dma_start(out=rw_bf[:], in_=res_weight.partition_broadcast(P))
-
         h_sb = const.tile([P, G * 8, H], BF16, name="h_sb")
+        w_sb = work.tile([P, 4, H], BF16, tag="hlg", align_bytes=64)
         adj_t = []
         y_t = []
         for g in range(G):
-            nc.sync.dma_start(
-                out=h_sb[:, 8 * g : 8 * g + 8, :], in_=h[g].rearrange("(t p) k -> p t k", p=P)
-            )
             a_tile = big.tile([P, 8, N], BF16, name="adj%d" % g, offset=(g + 1) * SLOT)
             adj_t.append(a_tile)
-            for hf in range(2):
+
+        def load_adj(g, v):
+            nc.sync.dma_start(
+                out=adj_t[g][:, 2 * v : 2 * v + 2, :],
+                in_=adj[g, 256 * v : 256 * v + 256, :].rearrange("(p e) n -> p e n", e=2),
+            )
+
+        def load_h(g, c):
+            for v in (2 * c, 2 * c + 1):
                 nc.sync.dma_start(
-                    out=a_tile[:, 4 * hf : 4 * hf + 4, :],
-                    in_=adj[g, 512 * hf : 512 * hf + 512, :].rearrange("(t p) n -> p t n", p=P),
+                    out=h_sb[:, 8 * g + 2 * v : 8 * g + 2 * v + 2, :],
+                    in_=h[g, 256 * v : 256 * v + 256, :].rearrange("(p e) k -> p e k", e=2),
                 )
+
+        vt = const.tile([P, P], BF16, name="vt")
+        nc.vector.memset(vt[:], 0.0)
+        brow = const.tile([P, H + 16], BF16, name="brow")
+        nc.vector.memset(brow[:], 0.0)
+        ones = const.tile([P, P], BF16, name="ones")
+        nc.vector.memset(ones[:], 1.0)
+        warm = const.tile([P, 1], F32, name="warm")
+        nc.vector.memset(warm[:], 1.0)
+        nhalf = const.tile([P, 8], F32, name="nhalf")
+        nc.gpsimd.memset(nhalf[:], -0.5)
+
+        for v in range(4):
+            load_adj(0, v)
+        nc.sync.dma_start(out=w_sb[:], in_=W.rearrange("(a p) k -> p a k", p=P))
+        load_h(0, 0)
+        load_h(0, 1)
+        nc.scalar.dma_start(out=vt[0:4, :], in_=bn_weight.rearrange("(a p) -> a p", p=P))
+        nc.scalar.dma_start(out=vt[4:8, :], in_=bn_bias.rearrange("(a p) -> a p", p=P))
+        nc.scalar.dma_start(out=brow[0:1, 0:H], in_=b.unsqueeze(0))
+        nc.scalar.dma_start(out=brow[0:1, H : H + 1], in_=res_weight.unsqueeze(0))
+        nc.scalar.activation(out=warm[:], in_=warm[:], func=ACT.Sqrt)
+        for g in range(1, G):
+            for v in range(4):
+                load_adj(g, v)
+            load_h(g, 0)
+            load_h(g, 1)
+
+        ident_f = const.tile([P, P], F32, name="ident_f")
+        make_identity(nc, ident_f[:])
+        ident_bf = const.tile([P, P], BF16, name="ident_bf")
+        nc.gpsimd.tensor_copy(out=ident_bf[:], in_=ident_f[:])
+        spread = const.tile([P, 2, 2 * P], BF16, name="spread")
+        nc.gpsimd.memset(spread[:], 0.0)
+        for e in range(2):
+            nc.gpsimd.tensor_copy(out=spread[:, e, e : 2 * P : 2], in_=ident_f[:])
 
         wc = const.tile([P, H], U32, name="wc", align_bytes=64)
         ws = const.tile([P, H], U8, name="ws", align_bytes=64)
-        ysum = const.tile([P, 48], F32, name="ysum")
-        ysq = const.tile([P, 48], F32, name="ysq")
+        b_all = const.tile([P, H], F32, name="b_all")
+        ysum = const.tile([P, 8, 12], F32, name="ysum")
         negs = const.tile([P, 4], F32, name="negs")
         negr = const.tile([P, 4], F32, name="negr")
         bnv = const.tile([P, 8], F32, name="bnv")
         rw = const.tile([P, 1], F32, name="rw")
-        nc.vector.tensor_copy(out=rw[:], in_=rw_bf[:])
 
         state = {}
 
         with tc.psum_pool(name="ps1", bufs=2) as psum:
-            tpv = psum.tile([P, 8, P], BF16, tag="tp")
-            nc.tensor.transpose(tpv[:, 0, :], vt[:], ident_bf[:])
-            nc.vector.tensor_copy(out=bnv[:], in_=tpv[:, 0, 0:8])
 
-            def words_to_k(src_tiles, dst):
+            def deg_tile(g):
+                if ("deg", g) not in state:
+                    deg_new = small.tile([P, 8], F32, tag="deg", bufs=3)
+                    state[("deg", g)] = deg_new
+                return state[("deg", g)]
+
+            def deg_v(g, rt):
+                deg = deg_tile(g)
+                junk = work.tile([P, H], F32, tag="junkd", bufs=1)
+                nc.vector.scalar_tensor_tensor(
+                    out=junk[:],
+                    in0=adj_t[g][:, rt, 0:H],
+                    scalar=1.0,
+                    in1=adj_t[g][:, rt, H:N],
+                    op0=ALU.mult,
+                    op1=ALU.add,
+                    accum_out=deg[:, rt : rt + 1],
+                )
+
+            def deg_s(g, rt):
+                deg = deg_tile(g)
+                junk = work.tile([P, N], BF16, tag="junks", bufs=1)
+                nc.scalar.activation(
+                    out=junk[:], in_=adj_t[g][:, rt, :], func=ACT.Identity, accum_out=deg[:, rt : rt + 1]
+                )
+
+            def dis_chain(g):
+                deg = state[("deg", g)]
+                t0 = small.tile([P, 8], F32, tag="t0")
+                nc.gpsimd.tensor_scalar(
+                    out=t0[:], in0=deg[:], scalar1=1.0, scalar2=1e-30, op0=ALU.add, op1=ALU.max
+                )
+                mk = small.tile([P, 8], F32, tag="mk")
+                nc.gpsimd.tensor_scalar(
+                    out=mk[:], in0=deg[:], scalar1=1.0, scalar2=0.0, op0=ALU.add, op1=ALU.is_gt
+                )
+                r0 = small.tile([P, 8], F32, tag="r0")
+                nc.gpsimd.tensor_tensor(out=r0[:], in0=t0[:], in1=nhalf[:], op=ALU.pow)
+                dis = small.tile([P, 8], F32, tag="dis")
+                nc.gpsimd.tensor_tensor(out=dis[:], in0=r0[:], in1=mk[:], op=ALU.mult)
+                state[("dis", g)] = dis
+
+            def dis_spread(g):
+                dis = state[("dis", g)]
+                halves = []
+                for hf in range(2):
+                    ds = psum.tile([P, H], F32, tag="ds")
+                    for r in range(4):
+                        rt = 4 * hf + r
+                        lo = 2 * P * (r // 2)
+                        nc.tensor.transpose(
+                            ds[:, lo + r % 2 : lo + 2 * P : 2],
+                            dis[:, rt : rt + 1].to_broadcast([P, P]),
+                            ident_f[:],
+                        )
+                    halves.append(ds)
+                state[("ds", g)] = halves
+
+            def words_unit(src_a, src_b, dst, pr):
                 dstf = dst[:].bitcast(F32).rearrange("p (a n u) -> p a n u", a=4, u=2)
-                for pr in range(2):
-                    ps = psum.tile([P, 2, 2, P], F32, tag="tp")
-                    for a2 in range(2):
-                        for u in range(2):
-                            nc.tensor.transpose(
-                                ps[:, a2, u, :],
-                                src_tiles[2 * pr + a2].bitcast(F32)[:, P * u : P * u + P],
-                                ident_f[:],
-                            )
-                    nc.scalar.copy(
-                        out=dstf[:, 2 * pr : 2 * pr + 2], in_=ps[:].rearrange("p a u n -> p a n u")
-                    )
+                ps = psum.tile([P, 2, 2, P], F32, tag="tp")
+                for a2, src in enumerate((src_a, src_b)):
+                    for u in range(2):
+                        nc.tensor.transpose(
+                            ps[:, a2, u, :], src.bitcast(F32)[:, P * u : P * u + P], ident_f[:]
+                        )
+                nc.scalar.copy(
+                    out=dstf[:, 2 * pr : 2 * pr + 2], in_=ps[:].rearrange("p a u n -> p a n u")
+                )
 
-            wg = work.tile([P, 4 * H], BF16, tag="hg", align_bytes=64)
-            words_to_k([w_sb[:, a, :] for a in range(4)], wg)
-            nc.vector.quantize_mx(out=wc[:].bitcast(FP8X4), scales=ws[:], in_=wg[:])
-
-            def h_transpose(g, c):
-                hg = work.tile([P, 4 * H], BF16, tag="hg", align_bytes=64)
-                words_to_k([h_sb[:, 8 * g + 4 * c + t, :] for t in range(4)], hg)
-                state[("hg", g, c)] = hg
+            def h_unit(g, c, pr):
+                if pr == 0:
+                    hg_new = work.tile([P, 4 * H], BF16, tag="hg", align_bytes=64)
+                    state[("hg", g, c)] = hg_new
+                t = 8 * g + 4 * c + 2 * pr
+                words_unit(h_sb[:, t, :], h_sb[:, t + 1, :], state[("hg", g, c)], pr)
 
             def h_quant(g, c):
                 hc = work.tile([P, H], U32, tag="hc", align_bytes=64)
@@ -115,10 +187,6 @@ def tile_gcnlayer_t_kernel(tc, h, adj, W, b, bn_weight, bn_bias, res_weight, out
                 state[("hc", g, c)] = (hc, hs)
 
             def mm1(g, c, fc):
-                if fc == 0:
-                    hlg_new = work.tile([P, 4 * H], BF16, tag="hlg", align_bytes=64)
-                    state[("hlg", g, c)] = hlg_new
-                hlg = state[("hlg", g, c)]
                 hc, hs = state[("hc", g, c)]
                 m1 = psum.tile([P, 4, P], F32, tag="m1")
                 fs = slice(P * fc, P * fc + P)
@@ -133,6 +201,15 @@ def tile_gcnlayer_t_kernel(tc, h, adj, W, b, bn_weight, bn_bias, res_weight, out
                         start=True,
                         stop=True,
                     )
+                state[("m1", g, c, fc)] = m1
+
+            def mm1_out(g, c, fc):
+                if fc == 0:
+                    hlg_new = work.tile([P, 4 * H], BF16, tag="hlg", align_bytes=64)
+                    state[("hlg", g, c)] = hlg_new
+                hlg = state[("hlg", g, c)]
+                m1 = state[("m1", g, c, fc)]
+                fs = slice(P * fc, P * fc + P)
                 nc.vector.tensor_tensor(
                     out=hlg[:].rearrange("p (f t) -> p f t", t=4)[:, fs, :],
                     in0=m1[:].rearrange("p t f -> p f t"),
@@ -150,93 +227,25 @@ def tile_gcnlayer_t_kernel(tc, h, adj, W, b, bn_weight, bn_bias, res_weight, out
                     out=hlc[:, c, :].bitcast(FP8X4), scales=hls[:, c, :], in_=state[("hlg", g, c)][:]
                 )
 
-            def deg_row(g, rt):
-                if rt == 0:
-                    deg_new = small.tile([P, 8], F32, tag="deg")
-                    state[("deg", g)] = deg_new
-                deg = state[("deg", g)]
-                src = adj_t[g]
-                if g % 2 == 0:
-                    junk = work.tile([P, N], BF16, tag="junkd", bufs=1)
-                    nc.vector.tensor_scalar(
-                        out=junk[:],
-                        in0=src[:, rt, :],
-                        scalar1=1.0,
-                        scalar2=None,
-                        op0=ALU.mult,
-                        op1=ALU.add,
-                        accum_out=deg[:, rt : rt + 1],
-                    )
-                else:
-                    junk2 = work.tile([P, H], F32, tag="junkd", bufs=1)
-                    nc.vector.scalar_tensor_tensor(
-                        out=junk2[:],
-                        in0=src[:, rt, 0:H],
-                        scalar=1.0,
-                        in1=src[:, rt, H:N],
-                        op0=ALU.mult,
-                        op1=ALU.add,
-                        accum_out=deg[:, rt : rt + 1],
-                    )
-
-            def dis_chain(g):
-                deg = state[("deg", g)]
-                t0 = small.tile([P, 8], F32, tag="t0")
-                nc.vector.tensor_scalar(
-                    out=t0[:], in0=deg[:], scalar1=1.0, scalar2=1e-30, op0=ALU.add, op1=ALU.max
-                )
-                mk = small.tile([P, 8], F32, tag="mk")
-                nc.vector.tensor_scalar(
-                    out=mk[:], in0=deg[:], scalar1=1.0, scalar2=0.0, op0=ALU.add, op1=ALU.is_gt
-                )
-                sq = small.tile([P, 8], F32, tag="sq")
-                nc.scalar.activation(out=sq[:], in_=t0[:], func=ACT.Sqrt)
-                r0 = small.tile([P, 8], F32, tag="r0")
-                nc.vector.reciprocal(out=r0[:], in_=sq[:])
-                n1 = small.tile([P, 8], F32, tag="n1")
-                nc.vector.tensor_tensor(out=n1[:], in0=r0[:], in1=r0[:], op=ALU.mult)
-                n2 = small.tile([P, 8], F32, tag="n2")
-                nc.vector.tensor_tensor(out=n2[:], in0=n1[:], in1=t0[:], op=ALU.mult)
-                n3 = small.tile([P, 8], F32, tag="n3")
-                nc.vector.tensor_scalar(
-                    out=n3[:], in0=n2[:], scalar1=-0.5, scalar2=1.5, op0=ALU.mult, op1=ALU.add
-                )
-                n4 = small.tile([P, 8], F32, tag="n4")
-                nc.vector.tensor_tensor(out=n4[:], in0=r0[:], in1=n3[:], op=ALU.mult)
-                dis = small.tile([P, 8], F32, tag="dis")
-                nc.vector.tensor_tensor(out=dis[:], in0=n4[:], in1=mk[:], op=ALU.mult)
-                state[("dis", g)] = dis
-
-            def dis_spread(g):
-                dis = state[("dis", g)]
-                halves = []
-                for hf in range(2):
-                    ds = psum.tile([P, H], F32, tag="ds")
-                    for r in range(4):
-                        rt = 4 * hf + r
-                        nc.tensor.transpose(
-                            ds[:, P * r : P * r + P],
-                            dis[:, rt : rt + 1].to_broadcast([P, P]),
-                            ident_f[:],
-                        )
-                    halves.append(ds)
-                state[("ds", g)] = halves
-
-            def diag_block(g, rt):
-                a32 = work.tile([P, P], F32, tag="a32", bufs=4)
+            def diag_block(s):
+                g, rt = divmod(s, 8)
+                lo = 2 * P * (rt // 2)
+                a32 = work.tile([P, 2 * P], F32, tag="a32", bufs=3)
                 nc.gpsimd.tensor_tensor(
-                    out=a32[:], in0=adj_t[g][:, rt, P * rt : P * rt + P], in1=ident_bf[:], op=ALU.add
+                    out=a32[:], in0=adj_t[g][:, rt, lo : lo + 2 * P], in1=spread[:, rt % 2, :], op=ALU.add
                 )
-                state[("a32", g, rt)] = a32
+                state[("a32", s)] = a32
 
-            def a_scale(g, rt):
+            def a_scale(s):
+                g, rt = divmod(s, 8)
                 dis = state[("dis", g)]
                 halves = state[("ds", g)]
                 ah = work.tile([P, N], BF16, tag="ah", bufs=3)
-                cuts = sorted(set([0, P * rt, P * rt + P, H, N]))
+                d0 = 2 * P * (rt // 2)
+                cuts = sorted(set([0, d0, d0 + 2 * P, H, N]))
                 for lo, hi in zip(cuts[:-1], cuts[1:]):
-                    if lo == P * rt:
-                        src = state[("a32", g, rt)][:]
+                    if lo == d0:
+                        src = state[("a32", s)][:]
                     else:
                         src = adj_t[g][:, rt, lo:hi]
                     nc.vector.scalar_tensor_tensor(
@@ -247,185 +256,256 @@ def tile_gcnlayer_t_kernel(tc, h, adj, W, b, bn_weight, bn_bias, res_weight, out
                         op0=ALU.mult,
                         op1=ALU.mult,
                     )
-                tp = psum.tile([P, 8, P], BF16, tag="tp")
-                for s in range(8):
-                    nc.tensor.transpose(tp[:, s, :], ah[:, P * s : P * s + P], ident_bf[:])
-                ag = work.tile([P, 2, P, 4], BF16, tag="ag", bufs=3, align_bytes=64)
-                nc.scalar.copy(out=ag[:], in_=tp[:].rearrange("p (c t) m -> p c m t", c=2))
-                state[("ag", g, rt)] = ag
+                state[("ah", s)] = ah
 
-            def a_quant(g, rt):
-                r = rt % 4
-                if r == 0:
-                    ac_new = work.tile([P, 2, H], U32, tag="ac", align_bytes=64)
-                    as_new = work.tile([P, 2, H], U8, tag="as", align_bytes=64)
-                    state[("ac", g, rt // 4)] = (ac_new, as_new)
-                ac, asc = state[("ac", g, rt // 4)]
-                ag = state[("ag", g, rt)]
-                for c in range(2):
-                    nc.vector.quantize_mx(
-                        out=ac[:, c, P * r : P * r + P].bitcast(FP8X4),
-                        scales=asc[:, c, P * r : P * r + P],
-                        in_=ag[:, c].rearrange("p m t -> p (m t)"),
+            def a_transpose(s):
+                ah = state[("ah", s)]
+                tp = psum.tile([P, 4, P], F32, tag="tp")
+                for u in range(4):
+                    nc.tensor.transpose(
+                        tp[:, u, :], ah[:].bitcast(F32)[:, P * u : P * u + P], ident_f[:]
                     )
+                state[("tp", s)] = tp
 
-            def mm2(g, mh):
-                if mh == 0:
-                    y_new = big.tile([P, 4, N], F32, name="y%d" % g, offset=g * SLOT)
-                    y_t.append(y_new)
-                y = y_t[g]
-                ac, asc = state[("ac", g, mh)]
+            def a_copy(s):
+                if s % 2 == 0:
+                    ag_new = work.tile([P, 2 * 2 * P * 4], BF16, tag="ag", bufs=3, align_bytes=64)
+                    state[("ag", s // 2)] = ag_new
+                ag = state[("ag", s // 2)]
+                r0 = P * (s % 2)
+                nc.scalar.copy(
+                    out=ag[:].bitcast(F32).rearrange("p (c m u) -> p c m u", c=2, u=2)[:, :, r0 : r0 + P, :],
+                    in_=state[("tp", s)][:].rearrange("p (c u) m -> p c m u", c=2),
+                )
+
+            def a_quant(pair):
+                ac = work.tile([P, 4 * P], U32, tag="ac", bufs=4, align_bytes=64)
+                asc = work.tile([P, 4 * P], U8, tag="as", bufs=4, align_bytes=64)
+                nc.vector.quantize_mx(
+                    out=ac[:].bitcast(FP8X4), scales=asc[:], in_=state[("ag", pair)][:]
+                )
+                state[("ac", pair)] = (ac, asc)
+
+            def mm2(q, tag="m2"):
+                g, mh, fc = q // 8, (q // 4) % 2, q % 4
                 hlc, hls = state[("hlc", g)]
-                for fc in range(4):
-                    fs = slice(P * fc, P * fc + P)
-                    m2 = psum.tile([P, H], F32, tag="m2")
+                fs = slice(P * fc, P * fc + P)
+                m2 = psum.tile([P, H], F32, tag=tag)
+                for pr in range(2):
+                    ac, asc = state[("ac", 4 * g + 2 * mh + pr)]
                     for c in range(2):
+                        ms = slice(2 * P * c, 2 * P * c + 2 * P)
                         nc.tensor.matmul_mx(
-                            out=m2[:],
+                            out=m2[:, 2 * P * pr : 2 * P * pr + 2 * P],
                             lhsT=hlc[:, c, fs].bitcast(FP8X4),
                             lhsT_scale=hls[:, c, fs],
-                            rhs=ac[:, c, :].bitcast(FP8X4),
-                            rhs_scale=asc[:, c, :],
+                            rhs=ac[:, ms].bitcast(FP8X4),
+                            rhs_scale=asc[:, ms],
                             start=(c == 0),
                             stop=(c == 1),
                         )
-                    if g == 0 and mh == 0:
-                        nc.vector.tensor_reduce(
-                            out=negr[:, fc : fc + 1], in_=m2[:], axis=AX.X, op=ALU.add
-                        )
-                        nc.vector.tensor_scalar(
-                            out=negs[:, fc : fc + 1],
-                            in0=negr[:, fc : fc + 1],
-                            scalar1=-1.0 / H,
-                            scalar2=None,
-                            op0=ALU.mult,
-                        )
-                    idx = 12 * fc + 2 * g + mh
+                state[("m2", q)] = m2
+
+            def y_out(q, on_vector=False):
+                g, mh, fc = q // 8, (q // 4) % 2, q % 4
+                m2 = state[("m2", q)]
+                if q % 8 == 0:
+                    y_new = big.tile([P, 4, N], F32, name="y%d" % g, offset=g * SLOT)
+                    y_t.append(y_new)
+                if q < 4:
+                    nc.vector.tensor_reduce(
+                        out=negr[:, fc : fc + 1], in_=m2[:], axis=AX.X, op=ALU.add
+                    )
+                    nc.vector.tensor_scalar(
+                        out=negs[:, fc : fc + 1],
+                        in0=negr[:, fc : fc + 1],
+                        scalar1=-1.0 / H,
+                        scalar2=None,
+                        op0=ALU.mult,
+                    )
+                dst = y_t[g][:, fc, H * mh : H * mh + H]
+                acc = ysum[:, fc, 2 * g + mh : 2 * g + mh + 1]
+                if on_vector:
+                    nc.vector.tensor_scalar(
+                        out=dst,
+                        in0=m2[:],
+                        scalar1=negs[:, fc : fc + 1],
+                        scalar2=None,
+                        op0=ALU.add,
+                        op1=ALU.add,
+                        accum_out=acc,
+                    )
+                else:
                     nc.scalar.activation(
-                        out=y[:, fc, H * mh : H * mh + H],
+                        out=dst,
                         in_=m2[:],
                         func=ACT.Identity,
                         bias=negs[:, fc : fc + 1],
                         scale=1.0,
-                        accum_out=ysum[:, idx : idx + 1],
-                    )
-                    junks = work.tile([P, H], BF16, tag="junks", bufs=1)
-                    nc.scalar.activation(
-                        out=junks[:],
-                        in_=m2[:],
-                        func=ACT.Square,
-                        bias=negs[:, fc : fc + 1],
-                        scale=1.0,
-                        accum_out=ysq[:, idx : idx + 1],
+                        accum_out=acc,
                     )
 
-            def side_unit(g, i):
-                if i == 0:
-                    h_transpose(g, 0)
-                elif i == 1:
-                    h_quant(g, 0)
-                    h_transpose(g, 1)
-                elif i == 2:
-                    mm1(g, 0, 0)
-                    mm1(g, 0, 1)
-                    h_quant(g, 1)
-                elif i == 3:
-                    mm1(g, 0, 2)
-                    mm1(g, 0, 3)
-                elif i == 4:
+            def y_square(q):
+                g, mh, fc = q // 8, (q // 4) % 2, q % 4
+                junk = work.tile([P, N], BF16, tag="junks", bufs=1)
+                nc.scalar.activation(
+                    out=junk[:, 0:H],
+                    in_=state[("m2", q)][:],
+                    func=ACT.Square,
+                    bias=negs[:, fc : fc + 1],
+                    scale=1.0,
+                    accum_out=ysum[:, 4 + fc, 2 * g + mh : 2 * g + mh + 1],
+                )
+
+            for v in range(4):
+                deg_v(0, 2 * v)
+                deg_s(0, 2 * v + 1)
+            pb = psum.tile([P, H], F32, tag="m1")
+            nc.tensor.matmul(pb[:], lhsT=ones[:], rhs=brow[:, 0:H], start=True, stop=True)
+            nc.scalar.copy(out=b_all[:], in_=pb[:])
+            pr_ = psum.tile([P, 16], F32, tag="m1")
+            nc.tensor.matmul(pr_[:], lhsT=ones[:], rhs=brow[:, H : H + 16], start=True, stop=True)
+            nc.vector.tensor_copy(out=rw[:], in_=pr_[:, 0:1])
+            tpv = psum.tile([P, P], BF16, tag="m2")
+            nc.tensor.transpose(tpv[:], vt[:], ident_bf[:])
+            nc.vector.tensor_copy(out=bnv[:], in_=tpv[:, 0:8])
+            diag_block(0)
+            diag_block(1)
+            dis_chain(0)
+
+            wg = work.tile([P, 4 * H], BF16, tag="hg", align_bytes=64)
+            for pr in range(2):
+                words_unit(w_sb[:, 2 * pr, :], w_sb[:, 2 * pr + 1, :], wg, pr)
+            dis_spread(0)
+            for c in range(2):
+                for pr in range(2):
+                    if c == 1 and pr == 0:
+                        nc.vector.quantize_mx(out=wc[:].bitcast(FP8X4), scales=ws[:], in_=wg[:])
+                    h_unit(0, c, pr)
+
+            V_DEG = {1: (0, 1), 5: (2, 3)}
+            S_DEG = {2: (0, 6), 3: (0, 7), 6: (1, 4), 7: (1, 5)}
+            for s in range(8 * G):
+                g, rt = divmod(s, 8)
+                if s + 2 < 8 * G:
+                    diag_block(s + 2)
+                q = s - 5
+                if q >= 0:
+                    mm2(q)
+                units = []
+                if g == 0 and rt < 4:
+                    units = [(0, rt // 2, 2 * (rt % 2)), (0, rt // 2, 2 * (rt % 2) + 1)]
+                elif rt < 4:
+                    units = [(g, 1, rt)]
+                elif g + 1 < G:
+                    units = [(g + 1, 0, rt - 4)]
+
+                if s >= 1:
+                    a_copy(s - 1)
+                if q >= 0:
+                    y_out(q)
+                a_scale(s)
+                if s == 0:
+                    h_quant(0, 0)
+                    h_quant(0, 1)
+                if rt == 3 and g + 1 < G:
+                    h_quant(g + 1, 0)
+                if rt == 7 and g + 1 < G:
+                    h_quant(g + 1, 1)
+                for u in units:
+                    mm1(*u)
+                if g + 1 < G and rt in (1, 2, 5, 6):
+                    h_unit(g + 1, rt // 4, (rt - 1) % 4)
+                if q >= 0:
+                    y_square(q)
+                for u in units:
+                    mm1_out(*u)
+                if s % 2 == 0 and s >= 2:
+                    a_quant(s // 2 - 1)
+                if g > 0 and rt == 0:
                     hl_quant(g, 0)
-                    mm1(g, 1, 0)
-                    mm1(g, 1, 1)
-                elif i == 5:
-                    mm1(g, 1, 2)
-                    mm1(g, 1, 3)
-                elif i == 6:
+                if g == 0 and rt == 2:
+                    hl_quant(g, 0)
+                if rt == 4:
                     hl_quant(g, 1)
-                if i < 6:
-                    deg_row(g, i)
-                elif i == 6:
-                    deg_row(g, 6)
-                    deg_row(g, 7)
-                else:
-                    dis_chain(g)
+                if g + 1 < G and rt in V_DEG:
+                    for r in V_DEG[rt]:
+                        deg_v(g + 1, r)
+                if g == 0 and rt in (3, 4):
+                    deg_s(1, rt + 1)
+                if rt in S_DEG:
+                    ahead, r = S_DEG[rt]
+                    if g + 1 + ahead < G:
+                        deg_s(g + 1 + ahead, r)
+                if rt == 6 and g + 1 < G:
+                    dis_chain(g + 1)
+                a_transpose(s)
+                if rt == 7 and g + 1 < G:
+                    dis_spread(g + 1)
 
-            for i in range(8):
-                side_unit(0, i)
-            for g in range(G):
-                dis_spread(g)
-                diag_block(g, 0)
-                diag_block(g, 1)
-                for rt in range(8):
-                    if rt + 2 < 8:
-                        diag_block(g, rt + 2)
-                    a_scale(g, rt)
-                    if rt >= 1:
-                        a_quant(g, rt - 1)
-                    if rt == 4:
-                        mm2(g, 0)
-                    if g + 1 < G:
-                        side_unit(g + 1, rt)
-                a_quant(g, 7)
-                mm2(g, 1)
+            last = 8 * G
+            a_copy(last - 1)
+            for q in (last - 5,):
+                mm2(q)
+                y_out(q)
+                y_square(q)
+            a_quant(last // 2 - 1)
+            for i, q in enumerate(range(last - 4, last)):
+                mm2(q, tag=("m1", "m2")[i % 2])
+            for q in range(last - 4, last):
+                y_out(q, on_vector=True)
+            for q in range(last - 4, last):
+                y_square(q)
 
-        inv_n = 1.0 / (G * N)
-        s1 = small.tile([P, 4], F32, tag="s1")
-        nc.vector.tensor_reduce(
-            out=s1[:], in_=ysum[:].rearrange("p (f j) -> p f j", f=4), axis=AX.X, op=ALU.add
-        )
-        s2 = small.tile([P, 4], F32, tag="s2")
-        nc.vector.tensor_reduce(
-            out=s2[:], in_=ysq[:].rearrange("p (f j) -> p f j", f=4), axis=AX.X, op=ALU.add
-        )
-        mean = small.tile([P, 4], F32, tag="mean")
-        nc.vector.tensor_scalar(out=mean[:], in0=s1[:], scalar1=inv_n, scalar2=None, op0=ALU.mult)
-        ex2 = small.tile([P, 4], F32, tag="ex2")
-        nc.vector.tensor_scalar(
-            out=ex2[:], in0=s2[:], scalar1=inv_n, scalar2=BN_EPS, op0=ALU.mult, op1=ALU.add
-        )
+        cnt = float(G * N)
+        st = small.tile([P, 8], F32, tag="st")
+        nc.vector.tensor_reduce(out=st[:], in_=ysum[:], axis=AX.X, op=ALU.add)
         msq = small.tile([P, 4], F32, tag="msq")
-        nc.vector.tensor_tensor(out=msq[:], in0=mean[:], in1=mean[:], op=ALU.mult)
+        nc.vector.scalar_tensor_tensor(
+            out=msq[:], in0=st[:, 0:4], scalar=1.0 / cnt, in1=st[:, 0:4], op0=ALU.mult, op1=ALU.mult
+        )
         vpe = small.tile([P, 4], F32, tag="vpe")
-        nc.vector.tensor_tensor(out=vpe[:], in0=ex2[:], in1=msq[:], op=ALU.subtract)
+        nc.vector.scalar_tensor_tensor(
+            out=vpe[:], in0=st[:, 4:8], scalar=BN_EPS * cnt, in1=msq[:], op0=ALU.add, op1=ALU.subtract
+        )
         std = small.tile([P, 4], F32, tag="std")
-        nc.scalar.activation(out=std[:], in_=vpe[:], func=ACT.Sqrt)
+        nc.scalar.activation(out=std[:], in_=vpe[:], func=ACT.Sqrt, scale=1.0 / cnt)
         rstd = small.tile([P, 4], F32, tag="rstd")
         nc.vector.reciprocal(out=rstd[:], in_=std[:])
         sc = small.tile([P, 4], F32, tag="sc")
         nc.vector.tensor_tensor(out=sc[:], in0=rstd[:], in1=bnv[:, 0:4], op=ALU.mult)
-        msc = small.tile([P, 4], F32, tag="msc")
-        nc.vector.tensor_tensor(out=msc[:], in0=mean[:], in1=sc[:], op=ALU.mult)
+        nms = small.tile([P, 4], F32, tag="nms")
+        nc.vector.scalar_tensor_tensor(
+            out=nms[:], in0=st[:, 0:4], scalar=-1.0 / cnt, in1=sc[:], op0=ALU.mult, op1=ALU.mult
+        )
         sh = small.tile([P, 4], F32, tag="sh")
-        nc.vector.tensor_tensor(out=sh[:], in0=bnv[:, 4:8], in1=msc[:], op=ALU.subtract)
+        nc.vector.tensor_tensor(out=sh[:], in0=nms[:], in1=bnv[:, 4:8], op=ALU.add)
 
-        with tc.psum_pool(name="ps2", bufs=4) as psum2:
-            for g in range(G):
+        with tc.psum_pool(name="ps2", bufs=6) as psum2:
+            for pair in range(4 * G):
+                g, v = divmod(pair, 4)
                 y = y_t[g]
-                for mh in range(2):
+                for fc in range(4):
+                    part = y[:, fc, 2 * P * v : 2 * P * v + 2 * P]
+                    nc.scalar.activation(
+                        out=part, in_=part, func=ACT.Relu, bias=sh[:, fc : fc + 1], scale=sc[:, fc : fc + 1]
+                    )
+                ot = big.tile([P, 2, H], F32, name="ot%d" % pair, offset=6 * SLOT + (pair % 4) * 4096)
+                for e in range(2):
+                    rt = 2 * v + e
+                    to = psum2.tile([P, H], F32, tag="to")
                     for fc in range(4):
-                        part = y[:, fc, H * mh : H * mh + H]
-                        nc.scalar.activation(
-                            out=part,
-                            in_=part,
-                            func=ACT.Relu,
-                            bias=sh[:, fc : fc + 1],
-                            scale=sc[:, fc : fc + 1],
+                        nc.tensor.transpose(
+                            to[:, P * fc : P * fc + P], y[:, fc, P * rt : P * rt + P], ident_f[:]
                         )
-                    for r in range(4):
-                        rt = 4 * mh + r
-                        to = psum2.tile([P, H], F32, tag="to")
-                        for fc in range(4):
-                            nc.tensor.transpose(
-                                to[:, P * fc : P * fc + P], y[:, fc, P * rt : P * rt + P], ident_f[:]
-                            )
-                        i = 8 * g + rt
-                        ot = big.tile([P, H], F32, name="ot%d" % i, offset=6 * SLOT + (i % 8) * 2048)
-                        nc.vector.scalar_tensor_tensor(
-                            out=ot[:],
-                            in0=h_sb[:, i, :],
-                            scalar=rw[:, 0:1],
-                            in1=to[:],
-                            op0=ALU.mult,
-                            op1=ALU.add,
-                        )
-                        nc.sync.dma_start(out=out[g, P * rt : P * rt + P, :], in_=ot[:])
+                    nc.vector.scalar_tensor_tensor(
+                        out=ot[:, e, :],
+                        in0=h_sb[:, 8 * g + rt, :],
+                        scalar=rw[:, 0:1],
+                        in1=to[:],
+                        op0=ALU.mult,
+                        op1=ALU.add,
+                    )
+                nc.sync.dma_start(
+                    out=out[g, 256 * v : 256 * v + 256, :].rearrange("(p e) k -> p e k", e=2), in_=ot[:]
+                )

@@ -109,7 +109,7 @@ def tile_gcnlayer_t_kernel(tc, h, adj, W, b, bn_weight, bn_bias, res_weight, out
 
             def deg_v(g, rt):
                 deg = deg_tile(g)
-                junk = work.tile([P, H], F32, tag="junkd", bufs=1)
+                junk = work.tile([P, H], BF16, tag="junkd")
                 nc.vector.scalar_tensor_tensor(
                     out=junk[:],
                     in0=adj_t[g][:, rt, 0:H],
@@ -347,9 +347,9 @@ def tile_gcnlayer_t_kernel(tc, h, adj, W, b, bn_weight, bn_bias, res_weight, out
 
             def y_square(q):
                 g, mh, fc = q // 8, (q // 4) % 2, q % 4
-                junk = work.tile([P, N], BF16, tag="junks", bufs=1)
+                junk = work.tile([P, H], BF16, tag="junkq")
                 nc.scalar.activation(
-                    out=junk[:, 0:H],
+                    out=junk[:],
                     in_=state[("m2", q)][:],
                     func=ACT.Square,
                     bias=negs[:, fc : fc + 1],
@@ -359,75 +359,86 @@ def tile_gcnlayer_t_kernel(tc, h, adj, W, b, bn_weight, bn_bias, res_weight, out
 
             for v in range(4):
                 deg_v(0, 2 * v)
-                deg_s(0, 2 * v + 1)
+                if v < 3:
+                    deg_s(0, 2 * v + 1)
+                else:
+                    deg_v(0, 2 * v + 1)
+            diag_block(0)
+            diag_block(1)
+            dis_chain(0)
+            dis_spread(0)
+            a_scale(0)
+            wg = work.tile([P, 4 * H], BF16, tag="hg", align_bytes=64)
+            for pr in range(2):
+                words_unit(w_sb[:, 2 * pr, :], w_sb[:, 2 * pr + 1, :], wg, pr)
+            nc.vector.quantize_mx(out=wc[:].bitcast(FP8X4), scales=ws[:], in_=wg[:])
+            for pr in range(2):
+                h_unit(0, 0, pr)
+            a_transpose(0)
             pb = psum.tile([P, H], F32, tag="m1")
             nc.tensor.matmul(pb[:], lhsT=ones[:], rhs=brow[:, 0:H], start=True, stop=True)
             nc.scalar.copy(out=b_all[:], in_=pb[:])
             pr_ = psum.tile([P, 16], F32, tag="m1")
             nc.tensor.matmul(pr_[:], lhsT=ones[:], rhs=brow[:, H : H + 16], start=True, stop=True)
-            nc.vector.tensor_copy(out=rw[:], in_=pr_[:, 0:1])
+            nc.scalar.copy(out=rw[:], in_=pr_[:, 0:1])
             tpv = psum.tile([P, P], BF16, tag="m2")
             nc.tensor.transpose(tpv[:], vt[:], ident_bf[:])
-            nc.vector.tensor_copy(out=bnv[:], in_=tpv[:, 0:8])
-            diag_block(0)
-            diag_block(1)
-            dis_chain(0)
-
-            wg = work.tile([P, 4 * H], BF16, tag="hg", align_bytes=64)
-            for pr in range(2):
-                words_unit(w_sb[:, 2 * pr, :], w_sb[:, 2 * pr + 1, :], wg, pr)
-            dis_spread(0)
-            for c in range(2):
-                for pr in range(2):
-                    if c == 1 and pr == 0:
-                        nc.vector.quantize_mx(out=wc[:].bitcast(FP8X4), scales=ws[:], in_=wg[:])
-                    h_unit(0, c, pr)
+            nc.scalar.copy(out=bnv[:], in_=tpv[:, 0:8])
 
             V_DEG = {1: (0, 1), 5: (2, 3)}
             S_DEG = {2: (0, 6), 3: (0, 7), 6: (1, 4), 7: (1, 5)}
+            FIRST = {6: (0,), 7: (1, 2), 8: (3,)}
             for s in range(8 * G):
                 g, rt = divmod(s, 8)
                 if s + 2 < 8 * G:
                     diag_block(s + 2)
-                q = s - 5
-                if q >= 0:
-                    mm2(q)
+                qs = FIRST.get(s, (s - 5,) if s >= 9 else ())
                 units = []
-                if g == 0 and rt < 4:
-                    units = [(0, rt // 2, 2 * (rt % 2)), (0, rt // 2, 2 * (rt % 2) + 1)]
-                elif rt < 4:
+                if g == 0 and rt in (2, 3, 4, 5):
+                    units = [(0, (rt - 2) // 2, 2 * (rt % 2)), (0, (rt - 2) // 2, 2 * (rt % 2) + 1)]
+                elif g > 0 and rt < 4:
                     units = [(g, 1, rt)]
-                elif g + 1 < G:
-                    units = [(g + 1, 0, rt - 4)]
+                if g + 1 < G and rt >= 4:
+                    units.append((g + 1, 0, rt - 4))
 
                 if s >= 1:
                     a_copy(s - 1)
-                if q >= 0:
+                    a_scale(s)
+                for q in qs:
+                    mm2(q)
                     y_out(q)
-                a_scale(s)
-                if s == 0:
+                if s == 1:
                     h_quant(0, 0)
-                    h_quant(0, 1)
                 if rt == 3 and g + 1 < G:
                     h_quant(g + 1, 0)
                 if rt == 7 and g + 1 < G:
                     h_quant(g + 1, 1)
+                if g == 0 and rt == 4:
+                    hl_quant(0, 0)
                 for u in units:
                     mm1(*u)
+                    if len(units) > 2:
+                        mm1_out(*u)
+                if s == 1:
+                    h_unit(0, 1, 0)
+                    h_unit(0, 1, 1)
                 if g + 1 < G and rt in (1, 2, 5, 6):
                     h_unit(g + 1, rt // 4, (rt - 1) % 4)
-                if q >= 0:
+                for q in qs:
                     y_square(q)
                 for u in units:
-                    mm1_out(*u)
+                    if len(units) <= 2:
+                        mm1_out(*u)
+                if s == 2:
+                    h_quant(0, 1)
                 if s % 2 == 0 and s >= 2:
                     a_quant(s // 2 - 1)
                 if g > 0 and rt == 0:
                     hl_quant(g, 0)
-                if g == 0 and rt == 2:
-                    hl_quant(g, 0)
-                if rt == 4:
+                if g > 0 and rt == 4:
                     hl_quant(g, 1)
+                if g == 0 and rt == 5:
+                    hl_quant(0, 1)
                 if g + 1 < G and rt in V_DEG:
                     for r in V_DEG[rt]:
                         deg_v(g + 1, r)
@@ -439,7 +450,8 @@ def tile_gcnlayer_t_kernel(tc, h, adj, W, b, bn_weight, bn_bias, res_weight, out
                         deg_s(g + 1 + ahead, r)
                 if rt == 6 and g + 1 < G:
                     dis_chain(g + 1)
-                a_transpose(s)
+                if s >= 1:
+                    a_transpose(s)
                 if rt == 7 and g + 1 < G:
                     dis_spread(g + 1)
 

@@ -25,7 +25,6 @@ BN_EPS = 1e-5
 def tile_gcnlayer_t_kernel(tc, h, adj, W, b, bn_weight, bn_bias, res_weight, out):
     nc = tc.nc
     with ExitStack() as ctx:
-        ctx.enter_context(tc.manual_schedule())
         const = ctx.enter_context(tc.tile_pool(name="const", bufs=1))
         big = ctx.enter_context(tc.tile_pool(name="big", bufs=1))
         work = ctx.enter_context(tc.tile_pool(name="work", bufs=2))
@@ -91,7 +90,7 @@ def tile_gcnlayer_t_kernel(tc, h, adj, W, b, bn_weight, bn_bias, res_weight, out
         wc = const.tile([P, H], U32, name="wc", align_bytes=64)
         ws = const.tile([P, H], U8, name="ws", align_bytes=64)
         b_all = const.tile([P, H], F32, name="b_all")
-        ysum = const.tile([P, 8, 12], F32, name="ysum")
+        ysum = const.tile([P, 8, 13], F32, name="ysum")
         negs = const.tile([P, 4], F32, name="negs")
         negr = const.tile([P, 4], F32, name="negr")
         bnv = const.tile([P, 8], F32, name="bnv")
@@ -118,6 +117,24 @@ def tile_gcnlayer_t_kernel(tc, h, adj, W, b, bn_weight, bn_bias, res_weight, out
                     op0=ALU.mult,
                     op1=ALU.add,
                     accum_out=deg[:, rt : rt + 1],
+                )
+
+            def deg_pe(g, rt):
+                part = psum.tile([P, P // 2], F32, tag="m1")
+                for j in range(16):
+                    nc.tensor.matmul(
+                        part[:],
+                        lhsT=ident_bf[:],
+                        rhs=adj_t[g][:, rt, 64 * j : 64 * j + 64],
+                        start=(j == 0),
+                        stop=(j == 15),
+                    )
+                state[("part", g, rt)] = part
+
+            def deg_pe_out(g, rt):
+                deg = deg_tile(g)
+                nc.vector.tensor_reduce(
+                    out=deg[:, rt : rt + 1], in_=state[("part", g, rt)][:], axis=AX.X, op=ALU.add
                 )
 
             def deg_s(g, rt):
@@ -286,12 +303,15 @@ def tile_gcnlayer_t_kernel(tc, h, adj, W, b, bn_weight, bn_bias, res_weight, out
                 )
                 state[("ac", pair)] = (ac, asc)
 
-            def mm2(q, tag="m2"):
+            def mm2(q, tag="m2", parts=(0, 1)):
                 g, mh, fc = q // 8, (q // 4) % 2, q % 4
                 hlc, hls = state[("hlc", g)]
                 fs = slice(P * fc, P * fc + P)
-                m2 = psum.tile([P, H], F32, tag=tag)
-                for pr in range(2):
+                if ("m2", q) not in state:
+                    m2_new = psum.tile([P, H], F32, tag=tag)
+                    state[("m2", q)] = m2_new
+                m2 = state[("m2", q)]
+                for pr in parts:
                     ac, asc = state[("ac", 4 * g + 2 * mh + pr)]
                     for c in range(2):
                         ms = slice(2 * P * c, 2 * P * c + 2 * P)
@@ -304,31 +324,30 @@ def tile_gcnlayer_t_kernel(tc, h, adj, W, b, bn_weight, bn_bias, res_weight, out
                             start=(c == 0),
                             stop=(c == 1),
                         )
-                state[("m2", q)] = m2
 
-            def y_out(q, on_vector=False):
+            def y_out(q, on_vector=False, lo=0, hi=H, col=0):
                 g, mh, fc = q // 8, (q // 4) % 2, q % 4
                 m2 = state[("m2", q)]
                 if q % 8 == 0:
                     y_new = big.tile([P, 4, N], F32, name="y%d" % g, offset=g * SLOT)
                     y_t.append(y_new)
                 if q < 4:
-                    nc.vector.tensor_reduce(
-                        out=negr[:, fc : fc + 1], in_=m2[:], axis=AX.X, op=ALU.add
+                    junk = work.tile([P, H], BF16, tag="junkq")
+                    nc.scalar.activation(
+                        out=junk[:], in_=m2[:], func=ACT.Identity, accum_out=negr[:, fc : fc + 1]
                     )
-                    nc.vector.tensor_scalar(
+                    nc.scalar.activation(
                         out=negs[:, fc : fc + 1],
-                        in0=negr[:, fc : fc + 1],
-                        scalar1=-1.0 / H,
-                        scalar2=None,
-                        op0=ALU.mult,
+                        in_=negr[:, fc : fc + 1],
+                        func=ACT.Identity,
+                        scale=-1.0 / H,
                     )
-                dst = y_t[g][:, fc, H * mh : H * mh + H]
-                acc = ysum[:, fc, 2 * g + mh : 2 * g + mh + 1]
+                dst = y_t[g][:, fc, H * mh + lo : H * mh + hi]
+                acc = ysum[:, fc, 2 * g + mh + col : 2 * g + mh + col + 1]
                 if on_vector:
                     nc.vector.tensor_scalar(
                         out=dst,
-                        in0=m2[:],
+                        in0=m2[:, lo:hi],
                         scalar1=negs[:, fc : fc + 1],
                         scalar2=None,
                         op0=ALU.add,
@@ -338,23 +357,23 @@ def tile_gcnlayer_t_kernel(tc, h, adj, W, b, bn_weight, bn_bias, res_weight, out
                 else:
                     nc.scalar.activation(
                         out=dst,
-                        in_=m2[:],
+                        in_=m2[:, lo:hi],
                         func=ACT.Identity,
                         bias=negs[:, fc : fc + 1],
                         scale=1.0,
                         accum_out=acc,
                     )
 
-            def y_square(q):
+            def y_square(q, lo=0, hi=H, col=0):
                 g, mh, fc = q // 8, (q // 4) % 2, q % 4
                 junk = work.tile([P, H], BF16, tag="junkq")
                 nc.scalar.activation(
-                    out=junk[:],
-                    in_=state[("m2", q)][:],
+                    out=junk[:, lo:hi],
+                    in_=state[("m2", q)][:, lo:hi],
                     func=ACT.Square,
                     bias=negs[:, fc : fc + 1],
                     scale=1.0,
-                    accum_out=ysum[:, 4 + fc, 2 * g + mh : 2 * g + mh + 1],
+                    accum_out=ysum[:, 4 + fc, 2 * g + mh + col : 2 * g + mh + col + 1],
                 )
 
             for v in range(4):
@@ -385,8 +404,7 @@ def tile_gcnlayer_t_kernel(tc, h, adj, W, b, bn_weight, bn_bias, res_weight, out
             nc.tensor.transpose(tpv[:], vt[:], ident_bf[:])
             nc.scalar.copy(out=bnv[:], in_=tpv[:, 0:8])
 
-            V_DEG = {1: (0, 1), 5: (2, 3)}
-            S_DEG = {2: (0, 6), 3: (0, 7), 6: (1, 4), 7: (1, 5)}
+            DEGS = {1: (("S", 1, 0),), 2: (("S", 1, 1), ("S", 1, 2),), 3: (("S", 1, 3), ("S", 1, 4),), 4: (("S", 1, 5), ("S", 1, 6),), 5: (("S", 1, 7),), 6: (("T", 2, 0),), 7: (("T", 2, 1),), 8: (("T", 2, 2),), 9: (("T", 2, 3),), 10: (("T", 2, 4),), 11: (("S", 2, 5), ("T", 2, 6),), 12: (("T", 2, 7),), 14: (("T", 3, 0),), 15: (("T", 3, 1),), 16: (("T", 3, 2),), 17: (("T", 3, 3),), 18: (("T", 3, 4),), 19: (("S", 3, 5), ("T", 3, 6),), 20: (("T", 3, 7),), 22: (("T", 4, 0),), 23: (("T", 4, 1),), 24: (("T", 4, 2),), 25: (("T", 4, 3),), 26: (("T", 4, 4),), 27: (("S", 4, 5), ("T", 4, 6),), 28: (("T", 4, 7),), 30: (("T", 5, 0),), 31: (("T", 5, 1),), 32: (("T", 5, 2),), 33: (("T", 5, 3),), 34: (("T", 5, 4),), 35: (("S", 5, 5), ("T", 5, 6),), 36: (("T", 5, 7),)}
             FIRST = {6: (0,), 7: (1, 2), 8: (3,)}
             for s in range(8 * G):
                 g, rt = divmod(s, 8)
@@ -419,6 +437,9 @@ def tile_gcnlayer_t_kernel(tc, h, adj, W, b, bn_weight, bn_bias, res_weight, out
                     mm1(*u)
                     if len(units) > 2:
                         mm1_out(*u)
+                for kind, dg, dr in DEGS.get(s, ()):
+                    if kind == "T":
+                        deg_pe(dg, dr)
                 if s == 1:
                     h_unit(0, 1, 0)
                     h_unit(0, 1, 1)
@@ -429,6 +450,9 @@ def tile_gcnlayer_t_kernel(tc, h, adj, W, b, bn_weight, bn_bias, res_weight, out
                 for u in units:
                     if len(units) <= 2:
                         mm1_out(*u)
+                for kind, dg, dr in DEGS.get(s, ()):
+                    if kind == "T":
+                        deg_pe_out(dg, dr)
                 if s == 2:
                     h_quant(0, 1)
                 if s % 2 == 0 and s >= 2:
@@ -439,15 +463,11 @@ def tile_gcnlayer_t_kernel(tc, h, adj, W, b, bn_weight, bn_bias, res_weight, out
                     hl_quant(g, 1)
                 if g == 0 and rt == 5:
                     hl_quant(0, 1)
-                if g + 1 < G and rt in V_DEG:
-                    for r in V_DEG[rt]:
-                        deg_v(g + 1, r)
-                if g == 0 and rt in (3, 4):
-                    deg_s(1, rt + 1)
-                if rt in S_DEG:
-                    ahead, r = S_DEG[rt]
-                    if g + 1 + ahead < G:
-                        deg_s(g + 1 + ahead, r)
+                for kind, dg, dr in DEGS.get(s, ()):
+                    if kind == "V":
+                        deg_v(dg, dr)
+                    elif kind == "S":
+                        deg_s(dg, dr)
                 if rt == 6 and g + 1 < G:
                     dis_chain(g + 1)
                 if s >= 1:
@@ -457,17 +477,24 @@ def tile_gcnlayer_t_kernel(tc, h, adj, W, b, bn_weight, bn_bias, res_weight, out
 
             last = 8 * G
             a_copy(last - 1)
-            for q in (last - 5,):
-                mm2(q)
-                y_out(q)
-                y_square(q)
-            a_quant(last // 2 - 1)
+            q = last - 5
+            mm2(q)
+            y_out(q, on_vector=True)
+            y_square(q)
             for i, q in enumerate(range(last - 4, last)):
-                mm2(q, tag=("m1", "m2")[i % 2])
+                mm2(q, tag=("m1", "m2")[i % 2], parts=(0,))
+            for q in range(last - 4, last - 2):
+                y_out(q, on_vector=True, hi=2 * P)
+                y_square(q, hi=2 * P)
+            a_quant(last // 2 - 1)
+            for q in range(last - 2, last):
+                y_out(q, on_vector=True, hi=2 * P)
+                y_square(q, hi=2 * P)
             for q in range(last - 4, last):
-                y_out(q, on_vector=True)
+                mm2(q, parts=(1,))
             for q in range(last - 4, last):
-                y_square(q)
+                y_out(q, on_vector=True, lo=2 * P, col=1)
+                y_square(q, lo=2 * P, col=1)
 
         cnt = float(G * N)
         st = small.tile([P, 8], F32, tag="st")
@@ -482,33 +509,46 @@ def tile_gcnlayer_t_kernel(tc, h, adj, W, b, bn_weight, bn_bias, res_weight, out
         )
         std = small.tile([P, 4], F32, tag="std")
         nc.scalar.activation(out=std[:], in_=vpe[:], func=ACT.Sqrt, scale=1.0 / cnt)
+        nmw = small.tile([P, 4], F32, tag="nmw")
+        nc.vector.scalar_tensor_tensor(
+            out=nmw[:], in0=st[:, 0:4], scalar=-1.0 / cnt, in1=bnv[:, 0:4], op0=ALU.mult, op1=ALU.mult
+        )
         rstd = small.tile([P, 4], F32, tag="rstd")
         nc.vector.reciprocal(out=rstd[:], in_=std[:])
         sc = small.tile([P, 4], F32, tag="sc")
         nc.vector.tensor_tensor(out=sc[:], in0=rstd[:], in1=bnv[:, 0:4], op=ALU.mult)
-        nms = small.tile([P, 4], F32, tag="nms")
-        nc.vector.scalar_tensor_tensor(
-            out=nms[:], in0=st[:, 0:4], scalar=-1.0 / cnt, in1=sc[:], op0=ALU.mult, op1=ALU.mult
-        )
         sh = small.tile([P, 4], F32, tag="sh")
-        nc.vector.tensor_tensor(out=sh[:], in0=nms[:], in1=bnv[:, 4:8], op=ALU.add)
+        for fc in range(4):
+            nc.vector.scalar_tensor_tensor(
+                out=sh[:, fc : fc + 1],
+                in0=rstd[:, fc : fc + 1],
+                scalar=nmw[:, fc : fc + 1],
+                in1=bnv[:, 4 + fc : 5 + fc],
+                op0=ALU.mult,
+                op1=ALU.add,
+            )
 
-        with tc.psum_pool(name="ps2", bufs=6) as psum2:
-            for pair in range(4 * G):
-                g, v = divmod(pair, 4)
-                y = y_t[g]
+        with tc.psum_pool(name="ps2", bufs=8) as psum2:
+            def norm(g, v, width):
                 for fc in range(4):
-                    part = y[:, fc, 2 * P * v : 2 * P * v + 2 * P]
+                    part = y_t[g][:, fc, 2 * P * v : 2 * P * v + width]
                     nc.scalar.activation(
                         out=part, in_=part, func=ACT.Relu, bias=sh[:, fc : fc + 1], scale=sc[:, fc : fc + 1]
                     )
+
+            for pair in range(4 * G):
+                g, v = divmod(pair, 4)
+                if pair < 2:
+                    norm(g, v, 2 * P)
+                elif pair % 2 == 0:
+                    norm(g, v, 4 * P)
                 ot = big.tile([P, 2, H], F32, name="ot%d" % pair, offset=6 * SLOT + (pair % 4) * 4096)
                 for e in range(2):
                     rt = 2 * v + e
                     to = psum2.tile([P, H], F32, tag="to")
                     for fc in range(4):
                         nc.tensor.transpose(
-                            to[:, P * fc : P * fc + P], y[:, fc, P * rt : P * rt + P], ident_f[:]
+                            to[:, P * fc : P * fc + P], y_t[g][:, fc, P * rt : P * rt + P], ident_f[:]
                         )
                     nc.vector.scalar_tensor_tensor(
                         out=ot[:, e, :],

@@ -91,6 +91,7 @@ def tile_gcnlayer_t_kernel(tc, h, adj, W, b, bn_weight, bn_bias, res_weight, out
         ws = const.tile([P, H], U8, name="ws", align_bytes=64)
         b_all = const.tile([P, H], F32, name="b_all")
         ysum = const.tile([P, 8, 13], F32, name="ysum")
+        nc.vector.memset(ysum[:], 0.0)
         negs = const.tile([P, 4], F32, name="negs")
         negr = const.tile([P, 4], F32, name="negr")
         bnv = const.tile([P, 8], F32, name="bnv")
@@ -119,22 +120,23 @@ def tile_gcnlayer_t_kernel(tc, h, adj, W, b, bn_weight, bn_bias, res_weight, out
                     accum_out=deg[:, rt : rt + 1],
                 )
 
-            def deg_pe(g, rt):
-                part = psum.tile([P, P // 2], F32, tag="m1")
-                for j in range(16):
-                    nc.tensor.matmul(
-                        part[:],
-                        lhsT=ident_bf[:],
-                        rhs=adj_t[g][:, rt, 64 * j : 64 * j + 64],
-                        start=(j == 0),
-                        stop=(j == 15),
-                    )
-                state[("part", g, rt)] = part
+            def deg_pe(g, r0, rows):
+                part = psum.tile([P, rows, P // 2], F32, tag="m1")
+                for r in range(rows):
+                    for j in range(16):
+                        nc.tensor.matmul(
+                            part[:, r, :],
+                            lhsT=ident_bf[:],
+                            rhs=adj_t[g][:, r0 + r, 64 * j : 64 * j + 64],
+                            start=(j == 0),
+                            stop=(j == 15),
+                        )
+                state[("part", g, r0)] = part
 
-            def deg_pe_out(g, rt):
+            def deg_pe_out(g, r0, rows):
                 deg = deg_tile(g)
                 nc.vector.tensor_reduce(
-                    out=deg[:, rt : rt + 1], in_=state[("part", g, rt)][:], axis=AX.X, op=ALU.add
+                    out=deg[:, r0 : r0 + rows], in_=state[("part", g, r0)][:], axis=AX.X, op=ALU.add
                 )
 
             def deg_s(g, rt):
@@ -366,13 +368,15 @@ def tile_gcnlayer_t_kernel(tc, h, adj, W, b, bn_weight, bn_bias, res_weight, out
 
             def y_square(q, lo=0, hi=H, col=0):
                 g, mh, fc = q // 8, (q // 4) % 2, q % 4
-                junk = work.tile([P, H], BF16, tag="junkq")
+                if g < G - 1:
+                    if mh == 0:
+                        return
+                    lo = -H
+                junk = work.tile([P, N], BF16, tag="junkq")
                 nc.scalar.activation(
-                    out=junk[:, lo:hi],
-                    in_=state[("m2", q)][:, lo:hi],
+                    out=junk[:, 0 : hi - lo],
+                    in_=y_t[g][:, fc, H * mh + lo : H * mh + hi],
                     func=ACT.Square,
-                    bias=negs[:, fc : fc + 1],
-                    scale=1.0,
                     accum_out=ysum[:, 4 + fc, 2 * g + mh + col : 2 * g + mh + col + 1],
                 )
 
@@ -404,10 +408,12 @@ def tile_gcnlayer_t_kernel(tc, h, adj, W, b, bn_weight, bn_bias, res_weight, out
             nc.tensor.transpose(tpv[:], vt[:], ident_bf[:])
             nc.scalar.copy(out=bnv[:], in_=tpv[:, 0:8])
 
-            DEGS = {1: (("S", 1, 0),), 2: (("S", 1, 1), ("S", 1, 2),), 3: (("S", 1, 3), ("S", 1, 4),), 4: (("S", 1, 5), ("S", 1, 6),), 5: (("S", 1, 7),), 6: (("T", 2, 0),), 7: (("T", 2, 1),), 8: (("T", 2, 2),), 9: (("T", 2, 3),), 10: (("T", 2, 4),), 11: (("S", 2, 5), ("T", 2, 6),), 12: (("T", 2, 7),), 14: (("T", 3, 0),), 15: (("T", 3, 1),), 16: (("T", 3, 2),), 17: (("T", 3, 3),), 18: (("T", 3, 4),), 19: (("S", 3, 5), ("T", 3, 6),), 20: (("T", 3, 7),), 22: (("T", 4, 0),), 23: (("T", 4, 1),), 24: (("T", 4, 2),), 25: (("T", 4, 3),), 26: (("T", 4, 4),), 27: (("S", 4, 5), ("T", 4, 6),), 28: (("T", 4, 7),), 30: (("T", 5, 0),), 31: (("T", 5, 1),), 32: (("T", 5, 2),), 33: (("T", 5, 3),), 34: (("T", 5, 4),), 35: (("S", 5, 5), ("T", 5, 6),), 36: (("T", 5, 7),)}
+            T_ROWS = {0: (0, 3), 3: (3, 3)}
+            S_ROWS = ({1: (0,), 2: (1, 2), 3: (3, 4), 4: (5, 6), 5: (7,)}, {1: (6,), 3: (7,)})
             FIRST = {6: (0,), 7: (1, 2), 8: (3,)}
             for s in range(8 * G):
                 g, rt = divmod(s, 8)
+                more = g + 1 < G
                 if s + 2 < 8 * G:
                     diag_block(s + 2)
                 qs = FIRST.get(s, (s - 5,) if s >= 9 else ())
@@ -437,9 +443,8 @@ def tile_gcnlayer_t_kernel(tc, h, adj, W, b, bn_weight, bn_bias, res_weight, out
                     mm1(*u)
                     if len(units) > 2:
                         mm1_out(*u)
-                for kind, dg, dr in DEGS.get(s, ()):
-                    if kind == "T":
-                        deg_pe(dg, dr)
+                if g > 0 and more and rt in T_ROWS:
+                    deg_pe(g + 1, *T_ROWS[rt])
                 if s == 1:
                     h_unit(0, 1, 0)
                     h_unit(0, 1, 1)
@@ -450,9 +455,8 @@ def tile_gcnlayer_t_kernel(tc, h, adj, W, b, bn_weight, bn_bias, res_weight, out
                 for u in units:
                     if len(units) <= 2:
                         mm1_out(*u)
-                for kind, dg, dr in DEGS.get(s, ()):
-                    if kind == "T":
-                        deg_pe_out(dg, dr)
+                if g > 0 and more and rt in T_ROWS:
+                    deg_pe_out(g + 1, *T_ROWS[rt])
                 if s == 2:
                     h_quant(0, 1)
                 if s % 2 == 0 and s >= 2:
@@ -463,11 +467,8 @@ def tile_gcnlayer_t_kernel(tc, h, adj, W, b, bn_weight, bn_bias, res_weight, out
                     hl_quant(g, 1)
                 if g == 0 and rt == 5:
                     hl_quant(0, 1)
-                for kind, dg, dr in DEGS.get(s, ()):
-                    if kind == "V":
-                        deg_v(dg, dr)
-                    elif kind == "S":
-                        deg_s(dg, dr)
+                for r in S_ROWS[g > 0].get(rt, ()) if more else ():
+                    deg_s(g + 1, r)
                 if rt == 6 and g + 1 < G:
                     dis_chain(g + 1)
                 if s >= 1:
@@ -532,9 +533,22 @@ def tile_gcnlayer_t_kernel(tc, h, adj, W, b, bn_weight, bn_bias, res_weight, out
             def norm(g, v, width):
                 for fc in range(4):
                     part = y_t[g][:, fc, 2 * P * v : 2 * P * v + width]
-                    nc.scalar.activation(
-                        out=part, in_=part, func=ACT.Relu, bias=sh[:, fc : fc + 1], scale=sc[:, fc : fc + 1]
-                    )
+                    if g == 0 and v == 0 and fc >= 2:
+                        nc.vector.tensor_scalar(
+                            out=part,
+                            in0=part,
+                            scalar1=sc[:, fc : fc + 1],
+                            scalar2=sh[:, fc : fc + 1],
+                            op0=ALU.mult,
+                            op1=ALU.add,
+                        )
+                        nc.vector.tensor_scalar(
+                            out=part, in0=part, scalar1=0.0, scalar2=None, op0=ALU.max
+                        )
+                    else:
+                        nc.scalar.activation(
+                            out=part, in_=part, func=ACT.Relu, bias=sh[:, fc : fc + 1], scale=sc[:, fc : fc + 1]
+                        )
 
             for pair in range(4 * G):
                 g, v = divmod(pair, 4)
@@ -558,6 +572,12 @@ def tile_gcnlayer_t_kernel(tc, h, adj, W, b, bn_weight, bn_bias, res_weight, out
                         op0=ALU.mult,
                         op1=ALU.add,
                     )
-                nc.sync.dma_start(
-                    out=out[g, 256 * v : 256 * v + 256, :].rearrange("(p e) k -> p e k", e=2), in_=ot[:]
-                )
+                    if pair == 4 * G - 1:
+                        nc.sync.dma_start(
+                            out=out[g, 256 * v : 256 * v + 256, :].rearrange("(p e) k -> p e k", e=2)[:, e, :],
+                            in_=ot[:, e, :],
+                        )
+                if pair < 4 * G - 1:
+                    nc.sync.dma_start(
+                        out=out[g, 256 * v : 256 * v + 256, :].rearrange("(p e) k -> p e k", e=2), in_=ot[:]
+                    )

@@ -31,7 +31,7 @@ def tile_gcnlayer_t_kernel(tc, h, adj, W, b, bn_weight, bn_bias, res_weight, out
         small = ctx.enter_context(tc.tile_pool(name="small", bufs=2))
 
         h_sb = const.tile([P, G * 8, H], BF16, name="h_sb")
-        w_sb = work.tile([P, 4, H], BF16, tag="hlg", align_bytes=64)
+        w_sb = work.tile([P, 4, H], BF16, tag="hlg", bufs=1, align_bytes=64)
         adj_t = []
         y_t = []
         for g in range(G):
@@ -146,6 +146,24 @@ def tile_gcnlayer_t_kernel(tc, h, adj, W, b, bn_weight, bn_bias, res_weight, out
                     out=junk[:], in_=adj_t[g][:, rt, :], func=ACT.Identity, accum_out=deg[:, rt : rt + 1]
                 )
 
+            def dis_first(g):
+                deg = state[("deg", g)]
+                t0 = small.tile([P, 8], F32, tag="t0")
+                nc.vector.tensor_scalar(
+                    out=t0[:], in0=deg[:], scalar1=1.0, scalar2=1e-30, op0=ALU.add, op1=ALU.max
+                )
+                mk = small.tile([P, 8], F32, tag="mk")
+                nc.vector.tensor_scalar(
+                    out=mk[:], in0=deg[:], scalar1=1.0, scalar2=0.0, op0=ALU.add, op1=ALU.is_gt
+                )
+                sq = small.tile([P, 8], F32, tag="sq")
+                nc.scalar.activation(out=sq[:], in_=t0[:], func=ACT.Sqrt)
+                r0 = small.tile([P, 8], F32, tag="r0")
+                nc.vector.reciprocal(out=r0[:], in_=sq[:])
+                dis = small.tile([P, 8], F32, tag="dis")
+                nc.vector.tensor_tensor(out=dis[:], in0=r0[:], in1=mk[:], op=ALU.mult)
+                state[("dis", g)] = dis
+
             def dis_chain(g):
                 deg = state[("deg", g)]
                 t0 = small.tile([P, 8], F32, tag="t0")
@@ -223,27 +241,27 @@ def tile_gcnlayer_t_kernel(tc, h, adj, W, b, bn_weight, bn_bias, res_weight, out
                 state[("m1", g, c, fc)] = m1
 
             def mm1_out(g, c, fc):
-                if fc == 0:
-                    hlg_new = work.tile([P, 4 * H], BF16, tag="hlg", align_bytes=64)
-                    state[("hlg", g, c)] = hlg_new
-                hlg = state[("hlg", g, c)]
+                if fc == 0 and c == 0:
+                    hlg_new = work.tile([P, 2, 4 * H], BF16, tag="hlg", bufs=1, align_bytes=64)
+                    state[("hlg", g)] = hlg_new
+                hlg = state[("hlg", g)][:, c, :]
                 m1 = state[("m1", g, c, fc)]
                 fs = slice(P * fc, P * fc + P)
                 nc.vector.tensor_tensor(
-                    out=hlg[:].rearrange("p (f t) -> p f t", t=4)[:, fs, :],
+                    out=hlg.rearrange("p (f t) -> p f t", t=4)[:, fs, :],
                     in0=m1[:].rearrange("p t f -> p f t"),
                     in1=b_all[:, fs].unsqueeze(2).to_broadcast([P, P, 4]),
                     op=ALU.add,
                 )
 
-            def hl_quant(g, c):
-                if c == 0:
-                    hlc_new = work.tile([P, 2, H], U32, tag="hlc", align_bytes=64)
-                    hls_new = work.tile([P, 2, H], U8, tag="hls", align_bytes=64)
-                    state[("hlc", g)] = (hlc_new, hls_new)
-                hlc, hls = state[("hlc", g)]
+            def hl_quant(g):
+                hlc = work.tile([P, 2, H], U32, tag="hlc", align_bytes=64)
+                hls = work.tile([P, 2, H], U8, tag="hls", align_bytes=64)
+                state[("hlc", g)] = (hlc, hls)
                 nc.vector.quantize_mx(
-                    out=hlc[:, c, :].bitcast(FP8X4), scales=hls[:, c, :], in_=state[("hlg", g, c)][:]
+                    out=hlc[:].rearrange("p c f -> p (c f)").bitcast(FP8X4),
+                    scales=hls[:].rearrange("p c f -> p (c f)"),
+                    in_=state[("hlg", g)][:].rearrange("p c f -> p (c f)"),
                 )
 
             def diag_block(s):
@@ -388,7 +406,7 @@ def tile_gcnlayer_t_kernel(tc, h, adj, W, b, bn_weight, bn_bias, res_weight, out
                     deg_v(0, 2 * v + 1)
             diag_block(0)
             diag_block(1)
-            dis_chain(0)
+            dis_first(0)
             dis_spread(0)
             a_scale(0)
             wg = work.tile([P, 4 * H], BF16, tag="hg", align_bytes=64)
@@ -437,8 +455,6 @@ def tile_gcnlayer_t_kernel(tc, h, adj, W, b, bn_weight, bn_bias, res_weight, out
                     h_quant(g + 1, 0)
                 if rt == 7 and g + 1 < G:
                     h_quant(g + 1, 1)
-                if g == 0 and rt == 4:
-                    hl_quant(0, 0)
                 for u in units:
                     mm1(*u)
                     if len(units) > 2:
@@ -461,12 +477,10 @@ def tile_gcnlayer_t_kernel(tc, h, adj, W, b, bn_weight, bn_bias, res_weight, out
                     h_quant(0, 1)
                 if s % 2 == 0 and s >= 2:
                     a_quant(s // 2 - 1)
-                if g > 0 and rt == 0:
-                    hl_quant(g, 0)
                 if g > 0 and rt == 4:
-                    hl_quant(g, 1)
+                    hl_quant(g)
                 if g == 0 and rt == 5:
-                    hl_quant(0, 1)
+                    hl_quant(0)
                 for r in S_ROWS[g > 0].get(rt, ()) if more else ():
                     deg_s(g + 1, r)
                 if rt == 6 and g + 1 < G:

@@ -41,7 +41,7 @@ def tile_gcnlayer_t_kernel(tc, h, adj, W, b, bn_weight, bn_bias, res_weight, out
         def load_adj(g, v):
             nc.sync.dma_start(
                 out=adj_t[g][:, 2 * v : 2 * v + 2, :],
-                in_=adj[g, 256 * v : 256 * v + 256, :].rearrange("(p e) n -> p e n", e=2),
+                in_=adj[g, 256 * v : 256 * v + 256, :].rearrange("(e p) n -> p e n", e=2),
             )
 
         def load_h(g, c):
@@ -50,6 +50,11 @@ def tile_gcnlayer_t_kernel(tc, h, adj, W, b, bn_weight, bn_bias, res_weight, out
                     out=h_sb[:, 8 * g + 2 * v : 8 * g + 2 * v + 2, :],
                     in_=h[g, 256 * v : 256 * v + 256, :].rearrange("(p e) k -> p e k", e=2),
                 )
+
+        def reload_h(g):
+            nc.sync.dma_start(
+                out=h_sb[:, 8 * g : 8 * g + 8, :], in_=h[g].rearrange("(t p) k -> p t k", p=P)
+            )
 
         vt = const.tile([P, P], BF16, name="vt")
         nc.vector.memset(vt[:], 0.0)
@@ -82,10 +87,6 @@ def tile_gcnlayer_t_kernel(tc, h, adj, W, b, bn_weight, bn_bias, res_weight, out
         make_identity(nc, ident_f[:])
         ident_bf = const.tile([P, P], BF16, name="ident_bf")
         nc.gpsimd.tensor_copy(out=ident_bf[:], in_=ident_f[:])
-        spread = const.tile([P, 2, 2 * P], BF16, name="spread")
-        nc.gpsimd.memset(spread[:], 0.0)
-        for e in range(2):
-            nc.gpsimd.tensor_copy(out=spread[:, e, e : 2 * P : 2], in_=ident_f[:])
 
         wc = const.tile([P, H], U32, name="wc", align_bytes=64)
         ws = const.tile([P, H], U8, name="ws", align_bytes=64)
@@ -187,9 +188,8 @@ def tile_gcnlayer_t_kernel(tc, h, adj, W, b, bn_weight, bn_bias, res_weight, out
                     ds = psum.tile([P, H], F32, tag="ds")
                     for r in range(4):
                         rt = 4 * hf + r
-                        lo = 2 * P * (r // 2)
                         nc.tensor.transpose(
-                            ds[:, lo + r % 2 : lo + 2 * P : 2],
+                            ds[:, P * r : P * r + P],
                             dis[:, rt : rt + 1].to_broadcast([P, P]),
                             ident_f[:],
                         )
@@ -266,10 +266,9 @@ def tile_gcnlayer_t_kernel(tc, h, adj, W, b, bn_weight, bn_bias, res_weight, out
 
             def diag_block(s):
                 g, rt = divmod(s, 8)
-                lo = 2 * P * (rt // 2)
-                a32 = work.tile([P, 2 * P], F32, tag="a32", bufs=3)
+                a32 = work.tile([P, P], F32, tag="a32", bufs=3)
                 nc.gpsimd.tensor_tensor(
-                    out=a32[:], in0=adj_t[g][:, rt, lo : lo + 2 * P], in1=spread[:, rt % 2, :], op=ALU.add
+                    out=a32[:], in0=adj_t[g][:, rt, P * rt : P * rt + P], in1=ident_bf[:], op=ALU.add
                 )
                 state[("a32", s)] = a32
 
@@ -278,8 +277,8 @@ def tile_gcnlayer_t_kernel(tc, h, adj, W, b, bn_weight, bn_bias, res_weight, out
                 dis = state[("dis", g)]
                 halves = state[("ds", g)]
                 ah = work.tile([P, N], BF16, tag="ah", bufs=3)
-                d0 = 2 * P * (rt // 2)
-                cuts = sorted(set([0, d0, d0 + 2 * P, H, N]))
+                d0 = P * rt
+                cuts = sorted(set([0, d0, d0 + P, H, N]))
                 for lo, hi in zip(cuts[:-1], cuts[1:]):
                     if lo == d0:
                         src = state[("a32", s)][:]
@@ -466,6 +465,10 @@ def tile_gcnlayer_t_kernel(tc, h, adj, W, b, bn_weight, bn_bias, res_weight, out
                     h_unit(0, 1, 1)
                 if g + 1 < G and rt in (1, 2, 5, 6):
                     h_unit(g + 1, rt // 4, (rt - 1) % 4)
+                if s == 2:
+                    reload_h(0)
+                if g + 1 < G and rt == 7:
+                    reload_h(g + 1)
                 for q in qs:
                     y_square(q)
                 for u in units:
@@ -588,10 +591,10 @@ def tile_gcnlayer_t_kernel(tc, h, adj, W, b, bn_weight, bn_bias, res_weight, out
                     )
                     if pair == 4 * G - 1:
                         nc.sync.dma_start(
-                            out=out[g, 256 * v : 256 * v + 256, :].rearrange("(p e) k -> p e k", e=2)[:, e, :],
+                            out=out[g, 256 * v : 256 * v + 256, :].rearrange("(e p) k -> p e k", e=2)[:, e, :],
                             in_=ot[:, e, :],
                         )
                 if pair < 4 * G - 1:
                     nc.sync.dma_start(
-                        out=out[g, 256 * v : 256 * v + 256, :].rearrange("(p e) k -> p e k", e=2), in_=ot[:]
+                        out=out[g, 256 * v : 256 * v + 256, :].rearrange("(e p) k -> p e k", e=2), in_=ot[:]
                     )

from contextlib import ExitStack

import concourse.mybir as mybir
from concourse.masks import make_identity

FLOPS = 2 * 6144 * 512 * 512 + 2 * 6 * 1024 * 1024 * 512

F32 = mybir.dt.float32
BF16 = mybir.dt.bfloat16
U32 = mybir.dt.uint32
U8 = mybir.dt.uint8
FP8X4 = mybir.dt.float8_e4m3fn_x4
ALU = mybir.AluOpType
ACT = mybir.ActivationFunctionType
AX = mybir.AxisListType

P = 128
G = 6
N = 1024
H = 512
SLOT = 16384
BN_EPS = 1e-5


def tile_gcnlayer_t_kernel(tc, h, adj, W, b, bn_weight, bn_bias, res_weight, out):
    nc = tc.nc
    with ExitStack() as ctx:
        const = ctx.enter_context(tc.tile_pool(name="const", bufs=1))
        big = ctx.enter_context(tc.tile_pool(name="big", bufs=1))
        work = ctx.enter_context(tc.tile_pool(name="work", bufs=2))
        small = ctx.enter_context(tc.tile_pool(name="small", bufs=2))

        h_sb = const.tile([P, G * 8, H], BF16, name="h_sb")
        w_sb = work.tile([P, 4, H], BF16, tag="hlg", bufs=1, align_bytes=64)
        adj_t = []
        y_t = []
        for g in range(G):
            a_tile = big.tile([P, 8, N], BF16, name="adj%d" % g, offset=(g + 1) * SLOT)
            adj_t.append(a_tile)

        def load_adj(g, v):
            nc.sync.dma_start(
                out=adj_t[g][:, 2 * v : 2 * v + 2, :],
                in_=adj[g, 256 * v : 256 * v + 256, :].rearrange("(e p) n -> p e n", e=2),
            )

        def load_h(g, c):
            for v in (2 * c, 2 * c + 1):
                nc.sync.dma_start(
                    out=h_sb[:, 8 * g + 2 * v : 8 * g + 2 * v + 2, :],
                    in_=h[g, 256 * v : 256 * v + 256, :].rearrange("(p e) k -> p e k", e=2),
                )

        def reload_h(g):
            nc.sync.dma_start(
                out=h_sb[:, 8 * g : 8 * g + 8, :], in_=h[g].rearrange("(t p) k -> p t k", p=P)
            )

        vt = const.tile([P, P], BF16, name="vt")
        nc.vector.memset(vt[:], 0.0)
        brow = const.tile([P, H + 16], BF16, name="brow")
        nc.vector.memset(brow[:], 0.0)
        ones = const.tile([P, P], BF16, name="ones")
        nc.vector.memset(ones[:], 1.0)
        warm = const.tile([P, 1], F32, name="warm")
        nc.vector.memset(warm[:], 1.0)
        nhalf = const.tile([P, 8], F32, name="nhalf")
        nc.gpsimd.memset(nhalf[:], -0.5)

        for v in range(4):
            load_adj(0, v)
        nc.sync.dma_start(out=w_sb[:], in_=W.rearrange("(a p) k -> p a k", p=P))
        load_h(0, 0)
        load_h(0, 1)
        nc.scalar.dma_start(out=vt[0:4, :], in_=bn_weight.rearrange("(a p) -> a p", p=P))
        nc.scalar.dma_start(out=vt[4:8, :], in_=bn_bias.rearrange("(a p) -> a p", p=P))
        nc.scalar.dma_start(out=brow[0:1, 0:H], in_=b.unsqueeze(0))
        nc.scalar.dma_start(out=brow[0:1, H : H + 1], in_=res_weight.unsqueeze(0))
        nc.scalar.activation(out=warm[:], in_=warm[:], func=ACT.Sqrt)
        for g in range(1, G):
            for v in range(4):
                load_adj(g, v)
            load_h(g, 0)
            load_h(g, 1)

        ident_f = const.tile([P, P], F32, name="ident_f")
        make_identity(nc, ident_f[:])
        ident_bf = const.tile([P, P], BF16, name="ident_bf")
        nc.gpsimd.tensor_copy(out=ident_bf[:], in_=ident_f[:])

        wc = const.tile([P, H], U32, name="wc", align_bytes=64)
        ws = const.tile([P, H], U8, name="ws", align_bytes=64)
        b_all = const.tile([P, H], F32, name="b_all")
        ysum = const.tile([P, 8, 13], F32, name="ysum")
        nc.vector.memset(ysum[:], 0.0)
        negs = const.tile([P, 4], F32, name="negs")
        negr = const.tile([P, 4], F32, name="negr")
        bnv = const.tile([P, 8], F32, name="bnv")
        rw = const.tile([P, 1], F32, name="rw")

        state = {}

        with tc.psum_pool(name="ps1", bufs=2) as psum:

            def deg_tile(g):
                if ("deg", g) not in state:
                    deg_new = small.tile([P, 8], F32, tag="deg", bufs=3)
                    state[("deg", g)] = deg_new
                return state[("deg", g)]

            def deg_v(g, rt):
                deg = deg_tile(g)
                junk = work.tile([P, H], BF16, tag="junkd")
                nc.vector.scalar_tensor_tensor(
                    out=junk[:],
                    in0=adj_t[g][:, rt, 0:H],
                    scalar=1.0,
                    in1=adj_t[g][:, rt, H:N],
                    op0=ALU.mult,
                    op1=ALU.add,
                    accum_out=deg[:, rt : rt + 1],
                )

            def deg_pe(g, r0, rows):
                part = psum.tile([P, rows, P // 2], F32, tag="m1")
                for r in range(rows):
                    for j in range(16):
                        nc.tensor.matmul(
                            part[:, r, :],
                            lhsT=ident_bf[:],
                            rhs=adj_t[g][:, r0 + r, 64 * j : 64 * j + 64],
                            start=(j == 0),
                            stop=(j == 15),
                        )
                state[("part", g, r0)] = part

            def deg_pe_out(g, r0, rows):
                deg = deg_tile(g)
                nc.vector.tensor_reduce(
                    out=deg[:, r0 : r0 + rows], in_=state[("part", g, r0)][:], axis=AX.X, op=ALU.add
                )

            def deg_s(g, rt):
                deg = deg_tile(g)
                junk = work.tile([P, N], BF16, tag="junks", bufs=1)
                nc.scalar.activation(
                    out=junk[:], in_=adj_t[g][:, rt, :], func=ACT.Identity, accum_out=deg[:, rt : rt + 1]
                )

            def dis_first(g):
                deg = state[("deg", g)]
                t0 = small.tile([P, 8], F32, tag="t0")
                nc.vector.tensor_scalar(
                    out=t0[:], in0=deg[:], scalar1=1.0, scalar2=1e-30, op0=ALU.add, op1=ALU.max
                )
                mk = small.tile([P, 8], F32, tag="mk")
                nc.vector.tensor_scalar(
                    out=mk[:], in0=deg[:], scalar1=1.0, scalar2=0.0, op0=ALU.add, op1=ALU.is_gt
                )
                sq = small.tile([P, 8], F32, tag="sq")
                nc.scalar.activation(out=sq[:], in_=t0[:], func=ACT.Sqrt)
                r0 = small.tile([P, 8], F32, tag="r0")
                nc.vector.reciprocal(out=r0[:], in_=sq[:])
                dis = small.tile([P, 8], F32, tag="dis")
                nc.vector.tensor_tensor(out=dis[:], in0=r0[:], in1=mk[:], op=ALU.mult)
                state[("dis", g)] = dis

            def dis_chain(g):
                deg = state[("deg", g)]
                t0 = small.tile([P, 8], F32, tag="t0")
                nc.gpsimd.tensor_scalar(
                    out=t0[:], in0=deg[:], scalar1=1.0, scalar2=1e-30, op0=ALU.add, op1=ALU.max
                )
                mk = small.tile([P, 8], F32, tag="mk")
                nc.gpsimd.tensor_scalar(
                    out=mk[:], in0=deg[:], scalar1=1.0, scalar2=0.0, op0=ALU.add, op1=ALU.is_gt
                )
                r0 = small.tile([P, 8], F32, tag="r0")
                nc.gpsimd.tensor_tensor(out=r0[:], in0=t0[:], in1=nhalf[:], op=ALU.pow)
                dis = small.tile([P, 8], F32, tag="dis")
                nc.gpsimd.tensor_tensor(out=dis[:], in0=r0[:], in1=mk[:], op=ALU.mult)
                state[("dis", g)] = dis

            def dis_spread(g):
                dis = state[("dis", g)]
                halves = []
                for hf in range(2):
                    ds = psum.tile([P, H], F32, tag="ds")
                    for r in range(4):
                        rt = 4 * hf + r
                        nc.tensor.transpose(
                            ds[:, P * r : P * r + P],
                            dis[:, rt : rt + 1].to_broadcast([P, P]),
                            ident_f[:],
                        )
                    halves.append(ds)
                state[("ds", g)] = halves

            def words_unit(src_a, src_b, dst, pr):
                dstf = dst[:].bitcast(F32).rearrange("p (a n u) -> p a n u", a=4, u=2)
                ps = psum.tile([P, 2, 2, P], F32, tag="tp")
                for a2, src in enumerate((src_a, src_b)):
                    for u in range(2):
                        nc.tensor.transpose(
                            ps[:, a2, u, :], src.bitcast(F32)[:, P * u : P * u + P], ident_f[:]
                        )
                nc.scalar.copy(
                    out=dstf[:, 2 * pr : 2 * pr + 2], in_=ps[:].rearrange("p a u n -> p a n u")
                )

            def h_unit(g, c, pr):
                if pr == 0:
                    hg_new = work.tile([P, 4 * H], BF16, tag="hg", align_bytes=64)
                    state[("hg", g, c)] = hg_new
                t = 8 * g + 4 * c + 2 * pr
                words_unit(h_sb[:, t, :], h_sb[:, t + 1, :], state[("hg", g, c)], pr)

            def h_quant(g, c):
                hc = work.tile([P, H], U32, tag="hc", align_bytes=64)
                hs = work.tile([P, H], U8, tag="hs", align_bytes=64)
                nc.vector.quantize_mx(
                    out=hc[:].bitcast(FP8X4), scales=hs[:], in_=state[("hg", g, c)][:]
                )
                state[("hc", g, c)] = (hc, hs)

            def mm1(g, c, fc):
                hc, hs = state[("hc", g, c)]
                m1 = psum.tile([P, 4, P], F32, tag="m1")
                fs = slice(P * fc, P * fc + P)
                for t in range(4):
                    ts = slice(P * t, P * t + P)
                    nc.tensor.matmul_mx(
                        out=m1[:, t, :],
                        lhsT=hc[:, ts].bitcast(FP8X4),
                        lhsT_scale=hs[:, ts],
                        rhs=wc[:, fs].bitcast(FP8X4),
                        rhs_scale=ws[:, fs],
                        start=True,
                        stop=True,
                    )
                state[("m1", g, c, fc)] = m1

            def mm1_out(g, c, fc):
                if fc == 0 and c == 0:
                    hlg_new = work.tile([P, 2, 4 * H], BF16, tag="hlg", bufs=1, align_bytes=64)
                    state[("hlg", g)] = hlg_new
                hlg = state[("hlg", g)][:, c, :]
                m1 = state[("m1", g, c, fc)]
                fs = slice(P * fc, P * fc + P)
                nc.vector.tensor_tensor(
                    out=hlg.rearrange("p (f t) -> p f t", t=4)[:, fs, :],
                    in0=m1[:].rearrange("p t f -> p f t"),
                    in1=b_all[:, fs].unsqueeze(2).to_broadcast([P, P, 4]),
                    op=ALU.add,
                )

            def hl_quant(g):
                hlc = work.tile([P, 2, H], U32, tag="hlc", align_bytes=64)
                hls = work.tile([P, 2, H], U8, tag="hls", align_bytes=64)
                state[("hlc", g)] = (hlc, hls)
                nc.vector.quantize_mx(
                    out=hlc[:].rearrange("p c f -> p (c f)").bitcast(FP8X4),
                    scales=hls[:].rearrange("p c f -> p (c f)"),
                    in_=state[("hlg", g)][:].rearrange("p c f -> p (c f)"),
                )

            def diag_block(s):
                g, rt = divmod(s, 8)
                a32 = work.tile([P, P], F32, tag="a32", bufs=3)
                nc.gpsimd.tensor_tensor(
                    out=a32[:], in0=adj_t[g][:, rt, P * rt : P * rt + P], in1=ident_bf[:], op=ALU.add
                )
                state[("a32", s)] = a32

            def a_scale(s):
                g, rt = divmod(s, 8)
                dis = state[("dis", g)]
                halves = state[("ds", g)]
                ah = work.tile([P, N], BF16, tag="ah", bufs=3)
                d0 = P * rt
                cuts = sorted(set([0, d0, d0 + P, H, N]))
                for lo, hi in zip(cuts[:-1], cuts[1:]):
                    if lo == d0:
                        src = state[("a32", s)][:]
                    else:
                        src = adj_t[g][:, rt, lo:hi]
                    nc.vector.scalar_tensor_tensor(
                        out=ah[:, lo:hi],
                        in0=src,
                        scalar=dis[:, rt : rt + 1],
                        in1=halves[lo // H][:, lo % H : lo % H + hi - lo],
                        op0=ALU.mult,
                        op1=ALU.mult,
                    )
                state[("ah", s)] = ah

            def a_transpose(s):
                ah = state[("ah", s)]
                tp = psum.tile([P, 4, P], F32, tag="tp")
                for u in range(4):
                    nc.tensor.transpose(
                        tp[:, u, :], ah[:].bitcast(F32)[:, P * u : P * u + P], ident_f[:]
                    )
                state[("tp", s)] = tp

            def a_copy(s):
                if s % 2 == 0:
                    ag_new = work.tile([P, 2 * 2 * P * 4], BF16, tag="ag", bufs=3, align_bytes=64)
                    state[("ag", s // 2)] = ag_new
                ag = state[("ag", s // 2)]
                r0 = P * (s % 2)
                nc.scalar.copy(
                    out=ag[:].bitcast(F32).rearrange("p (c m u) -> p c m u", c=2, u=2)[:, :, r0 : r0 + P, :],
                    in_=state[("tp", s)][:].rearrange("p (c u) m -> p c m u", c=2),
                )

            def a_quant(pair):
                ac = work.tile([P, 4 * P], U32, tag="ac", bufs=4, align_bytes=64)
                asc = work.tile([P, 4 * P], U8, tag="as", bufs=4, align_bytes=64)
                nc.vector.quantize_mx(
                    out=ac[:].bitcast(FP8X4), scales=asc[:], in_=state[("ag", pair)][:]
                )
                state[("ac", pair)] = (ac, asc)

            def mm2(q, tag="m2", parts=(0, 1)):
                g, mh, fc = q // 8, (q // 4) % 2, q % 4
                hlc, hls = state[("hlc", g)]
                fs = slice(P * fc, P * fc + P)
                if ("m2", q) not in state:
                    m2_new = psum.tile([P, H], F32, tag=tag)
                    state[("m2", q)] = m2_new
                m2 = state[("m2", q)]
                for pr in parts:
                    ac, asc = state[("ac", 4 * g + 2 * mh + pr)]
                    for c in range(2):
                        ms = slice(2 * P * c, 2 * P * c + 2 * P)
                        nc.tensor.matmul_mx(
                            out=m2[:, 2 * P * pr : 2 * P * pr + 2 * P],
                            lhsT=hlc[:, c, fs].bitcast(FP8X4),
                            lhsT_scale=hls[:, c, fs],
                            rhs=ac[:, ms].bitcast(FP8X4),
                            rhs_scale=asc[:, ms],
                            start=(c == 0),
                            stop=(c == 1),
                        )

            def y_out(q, on_vector=False, lo=0, hi=H, col=0):
                g, mh, fc = q // 8, (q // 4) % 2, q % 4
                m2 = state[("m2", q)]
                if q % 8 == 0:
                    y_new = big.tile([P, 4, N], F32, name="y%d" % g, offset=g * SLOT)
                    y_t.append(y_new)
                if q < 4:
                    junk = work.tile([P, H], BF16, tag="junkq")
                    nc.scalar.activation(
                        out=junk[:], in_=m2[:], func=ACT.Identity, accum_out=negr[:, fc : fc + 1]
                    )
                    nc.scalar.activation(
                        out=negs[:, fc : fc + 1],
                        in_=negr[:, fc : fc + 1],
                        func=ACT.Identity,
                        scale=-1.0 / H,
                    )
                dst = y_t[g][:, fc, H * mh + lo : H * mh + hi]
                acc = ysum[:, fc, 2 * g + mh + col : 2 * g + mh + col + 1]
                if on_vector:
                    nc.vector.tensor_scalar(
                        out=dst,
                        in0=m2[:, lo:hi],
                        scalar1=negs[:, fc : fc + 1],
                        scalar2=None,
                        op0=ALU.add,
                        op1=ALU.add,
                        accum_out=acc,
                    )
                else:
                    nc.scalar.activation(
                        out=dst,
                        in_=m2[:, lo:hi],
                        func=ACT.Identity,
                        bias=negs[:, fc : fc + 1],
                        scale=1.0,
                        accum_out=acc,
                    )

            def y_square(q, lo=0, hi=H, col=0):
                g, mh, fc = q // 8, (q // 4) % 2, q % 4
                if g < G - 1:
                    if mh == 0:
                        return
                    lo = -H
                junk = work.tile([P, N], BF16, tag="junkq")
                nc.scalar.activation(
                    out=junk[:, 0 : hi - lo],
                    in_=y_t[g][:, fc, H * mh + lo : H * mh + hi],
                    func=ACT.Square,
                    accum_out=ysum[:, 4 + fc, 2 * g + mh + col : 2 * g + mh + col + 1],
                )

            for v in range(4):
                deg_v(0, 2 * v)
                if v < 3:
                    deg_s(0, 2 * v + 1)
                else:
                    deg_v(0, 2 * v + 1)
            diag_block(0)
            diag_block(1)
            dis_first(0)
            dis_spread(0)
            a_scale(0)
            wg = work.tile([P, 4 * H], BF16, tag="hg", align_bytes=64)
            for pr in range(2):
                words_unit(w_sb[:, 2 * pr, :], w_sb[:, 2 * pr + 1, :], wg, pr)
            nc.vector.quantize_mx(out=wc[:].bitcast(FP8X4), scales=ws[:], in_=wg[:])
            for pr in range(2):
                h_unit(0, 0, pr)
            a_transpose(0)
            pb = psum.tile([P, H], F32, tag="m1")
            nc.tensor.matmul(pb[:], lhsT=ones[:], rhs=brow[:, 0:H], start=True, stop=True)
            nc.scalar.copy(out=b_all[:], in_=pb[:])
            pr_ = psum.tile([P, 16], F32, tag="m1")
            nc.tensor.matmul(pr_[:], lhsT=ones[:], rhs=brow[:, H : H + 16], start=True, stop=True)
            nc.scalar.copy(out=rw[:], in_=pr_[:, 0:1])
            tpv = psum.tile([P, P], BF16, tag="m2")
            nc.tensor.transpose(tpv[:], vt[:], ident_bf[:])
            nc.scalar.copy(out=bnv[:], in_=tpv[:, 0:8])

            T_ROWS = {0: (0, 3), 3: (3, 3)}
            S_ROWS = ({1: (0,), 2: (1, 2), 3: (3, 4), 4: (5, 6), 5: (7,)}, {1: (6,), 3: (7,)})
            FIRST = {6: (0,), 7: (1, 2), 8: (3,)}
            for s in range(8 * G):
                g, rt = divmod(s, 8)
                more = g + 1 < G
                if s + 2 < 8 * G:
                    diag_block(s + 2)
                qs = FIRST.get(s, (s - 5,) if s >= 9 else ())
                units = []
                if g == 0 and rt in (2, 3, 4, 5):
                    units = [(0, (rt - 2) // 2, 2 * (rt % 2)), (0, (rt - 2) // 2, 2 * (rt % 2) + 1)]
                elif g > 0 and rt < 4:
                    units = [(g, 1, rt)]
                if g + 1 < G and rt >= 4:
                    units.append((g + 1, 0, rt - 4))

                if s >= 1:
                    a_copy(s - 1)
                    a_scale(s)
                for q in qs:
                    mm2(q)
                    y_out(q)
                if s == 1:
                    h_quant(0, 0)
                if rt == 3 and g + 1 < G:
                    h_quant(g + 1, 0)
                if rt == 7 and g + 1 < G:
                    h_quant(g + 1, 1)
                for u in units:
                    mm1(*u)
                    if len(units) > 2:
                        mm1_out(*u)
                if g > 0 and more and rt in T_ROWS:
                    deg_pe(g + 1, *T_ROWS[rt])
                if s == 1:
                    h_unit(0, 1, 0)
                    h_unit(0, 1, 1)
                if g + 1 < G and rt in (1, 2, 5, 6):
                    h_unit(g + 1, rt // 4, (rt - 1) % 4)
                if s == 2:
                    reload_h(0)
                if g + 1 < G and rt == 7:
                    reload_h(g + 1)
                for q in qs:
                    y_square(q)
                for u in units:
                    if len(units) <= 2:
                        mm1_out(*u)
                if g > 0 and more and rt in T_ROWS:
                    deg_pe_out(g + 1, *T_ROWS[rt])
                if s == 2:
                    h_quant(0, 1)
                if s % 2 == 0 and s >= 2:
                    a_quant(s // 2 - 1)
                if g > 0 and rt == 4:
                    hl_quant(g)
                if g == 0 and rt == 5:
                    hl_quant(0)
                for r in S_ROWS[g > 0].get(rt, ()) if more else ():
                    deg_s(g + 1, r)
                if rt == 6 and g + 1 < G:
                    dis_chain(g + 1)
                if s >= 1:
                    a_transpose(s)
                if rt == 7 and g + 1 < G:
                    dis_spread(g + 1)

            last = 8 * G
            a_copy(last - 1)
            q = last - 5
            mm2(q)
            y_out(q, on_vector=True)
            y_square(q)
            for i, q in enumerate(range(last - 4, last)):
                mm2(q, tag=("m1", "m2")[i % 2], parts=(0,))
            for q in range(last - 4, last - 2):
                y_out(q, on_vector=True, hi=2 * P)
                y_square(q, hi=2 * P)
            a_quant(last // 2 - 1)
            for q in range(last - 2, last):
                y_out(q, on_vector=True, hi=2 * P)
                y_square(q, hi=2 * P)
            for q in range(last - 4, last):
                mm2(q, parts=(1,))
            for q in range(last - 4, last):
                y_out(q, on_vector=True, lo=2 * P, col=1)
                y_square(q, lo=2 * P, col=1)

        cnt = float(G * N)
        st = small.tile([P, 8], F32, tag="st")
        nc.vector.tensor_reduce(out=st[:], in_=ysum[:], axis=AX.X, op=ALU.add)
        msq = small.tile([P, 4], F32, tag="msq")
        nc.vector.scalar_tensor_tensor(
            out=msq[:], in0=st[:, 0:4], scalar=1.0 / cnt, in1=st[:, 0:4], op0=ALU.mult, op1=ALU.mult
        )
        vpe = small.tile([P, 4], F32, tag="vpe")
        nc.vector.scalar_tensor_tensor(
            out=vpe[:], in0=st[:, 4:8], scalar=BN_EPS * cnt, in1=msq[:], op0=ALU.add, op1=ALU.subtract
        )
        std = small.tile([P, 4], F32, tag="std")
        nc.scalar.activation(out=std[:], in_=vpe[:], func=ACT.Sqrt, scale=1.0 / cnt)
        nmw = small.tile([P, 4], F32, tag="nmw")
        nc.vector.scalar_tensor_tensor(
            out=nmw[:], in0=st[:, 0:4], scalar=-1.0 / cnt, in1=bnv[:, 0:4], op0=ALU.mult, op1=ALU.mult
        )
        rstd = small.tile([P, 4], F32, tag="rstd")
        nc.vector.reciprocal(out=rstd[:], in_=std[:])
        sc = small.tile([P, 4], F32, tag="sc")
        nc.vector.tensor_tensor(out=sc[:], in0=rstd[:], in1=bnv[:, 0:4], op=ALU.mult)
        sh = small.tile([P, 4], F32, tag="sh")
        for fc in range(4):
            nc.vector.scalar_tensor_tensor(
                out=sh[:, fc : fc + 1],
                in0=rstd[:, fc : fc + 1],
                scalar=nmw[:, fc : fc + 1],
                in1=bnv[:, 4 + fc : 5 + fc],
                op0=ALU.mult,
                op1=ALU.add,
            )

        with tc.psum_pool(name="ps2", bufs=8) as psum2:
            def norm(g, v, width):
                for fc in range(4):
                    part = y_t[g][:, fc, 2 * P * v : 2 * P * v + width]
                    if g == 0 and v == 0 and fc >= 2:
                        nc.vector.tensor_scalar(
                            out=part,
                            in0=part,
                            scalar1=sc[:, fc : fc + 1],
                            scalar2=sh[:, fc : fc + 1],
                            op0=ALU.mult,
                            op1=ALU.add,
                        )
                        nc.vector.tensor_scalar(
                            out=part, in0=part, scalar1=0.0, scalar2=None, op0=ALU.max
                        )
                    else:
                        nc.scalar.activation(
                            out=part, in_=part, func=ACT.Relu, bias=sh[:, fc : fc + 1], scale=sc[:, fc : fc + 1]
                        )

            for pair in range(4 * G):
                g, v = divmod(pair, 4)
                if pair < 2:
                    norm(g, v, 2 * P)
                elif pair % 2 == 0:
                    norm(g, v, 4 * P)
                ot = big.tile([P, 2, H], F32, name="ot%d" % pair, offset=6 * SLOT + (pair % 4) * 4096)
                for e in range(2):
                    rt = 2 * v + e
                    to = psum2.tile([P, H], F32, tag="to")
                    for fc in range(4):
                        nc.tensor.transpose(
                            to[:, P * fc : P * fc + P], y_t[g][:, fc, P * rt : P * rt + P], ident_f[:]
                        )
                    nc.vector.scalar_tensor_tensor(
                        out=ot[:, e, :],
                        in0=h_sb[:, 8 * g + rt, :],
                        scalar=rw[:, 0:1],
                        in1=to[:],
                        op0=ALU.mult,
                        op1=ALU.add,
                    )
                    if pair == 4 * G - 1:
                        nc.sync.dma_start(
                            out=out[g, 256 * v : 256 * v + 256, :].rearrange("(e p) k -> p e k", e=2)[:, e, :],
                            in_=ot[:, e, :],
                        )
                if pair < 4 * G - 1:
                    nc.sync.dma_start(
                        out=out[g, 256 * v : 256 * v + 256, :].rearrange("(e p) k -> p e k", e=2), in_=ot[:]
                    )
